import numpy as np
import ml_dtypes


def mxq(x, axis, fmt="e4m3"):
    dtype, down = {"e4m3": (ml_dtypes.float8_e4m3fn, 7), "e5m2": (ml_dtypes.float8_e5m2, 14)}[fmt]
    v = np.moveaxis(np.asarray(x, np.float32).astype(ml_dtypes.bfloat16).astype(np.float64), axis, -1)
    blocks = v.reshape(v.shape[:-1] + (-1, 32))
    amax = np.abs(blocks).max(-1, keepdims=True)
    byte = np.maximum(np.where(amax > 0, np.frexp(amax)[1] - 1 + 127, 0) - down, 1)
    scale = np.exp2(byte - 127.0)
    codes = (blocks / scale).astype(np.float32).astype(dtype).astype(np.float64)
    return np.moveaxis((codes * scale).reshape(v.shape), -1, axis)


WIDE = False


def mx_kscale(k):
    if not WIDE:
        return np.ones(k)
    levels = np.array([10, -10, 5, -5, 0])
    if k % 512:
        return np.exp2(np.random.permutation(np.resize(levels, k // 32))).repeat(32)
    a = np.empty((k // 512, 16))
    for p in range(k // 512):
        a[p, :8] = np.random.permutation(np.resize(levels, 8))
        for g in range(8):
            far = levels[np.abs(levels - a[p, g]) >= 10]
            a[p, g + 8] = far[np.random.randint(len(far))]
    return np.exp2(a.ravel()).repeat(32)


BF16 = ml_dtypes.bfloat16


def bf(x):
    return np.asarray(x, np.float32).astype(BF16)


def f64(x):
    return np.asarray(x).astype(np.float64)


B, T, D, H, HD, F = 4, 1024, 512, 8, 64, 128
A = H * HD
EPS = 1e-5
ERF_H = 0.5
ERF_N = 14


def layernorm(x, g, b):
    mu = np.mean(x, axis=-1, keepdims=True)
    var = np.mean(np.square(x - mu), axis=-1, keepdims=True)
    return (x - mu) / np.sqrt(var + EPS) * g + b


def erf(z):
    acc = np.zeros_like(z)
    for n in range(ERF_N):
        tn = (n + 0.5) * ERF_H
        acc = acc + np.exp(-tn * tn) / (tn * tn + z * z)
    return np.tanh(np.pi * z / ERF_H) - 2.0 * ERF_H * z * np.exp(-z * z) / np.pi * acc


def gelu_erf(v):
    return 0.5 * v * (1.0 + erf(v / np.sqrt(2.0)))


def setup_inputs():
    s, t = mx_kscale(A), mx_kscale(D)
    return {"attn": bf(np.random.standard_normal((B, T, A)) * 0.25 * s),
            "x": bf(np.random.standard_normal((B, T, D)) + 0.5 * np.random.standard_normal((B, T, 1))),
            "w_out": bf(np.random.standard_normal((A, D)) * 2.0 / np.sqrt(A) / s[:, None]),
            "b_out": bf(0.1 * np.random.standard_normal(D)),
            "ln2_g": bf((1.0 + 0.1 * np.random.standard_normal(D)) * t),
            "ln2_b": bf(0.1 * np.random.standard_normal(D) * t),
            "w1": bf(np.random.standard_normal((D, F)) / np.sqrt(D) / t[:, None]),
            "b1": bf(0.2 * np.random.standard_normal(F))}


def reference(attn, x, w_out, b_out, ln2_g, ln2_b, w1, b1):
    x_mid = f64(x) + ((mxq(f64(attn), 2, "e4m3") @ mxq(f64(w_out), 0, "e4m3")) + f64(b_out))
    h2 = layernorm(x_mid, f64(ln2_g), f64(ln2_b))
    hid = gelu_erf((mxq(h2, 2, "e4m3") @ mxq(f64(w1), 0, "e4m3")) + f64(b1))
    return x_mid, hid

@@ -1,0 +1,294 @@
+from contextlib import ExitStack
+
+import concourse.mybir as mybir
+from concourse.masks import make_identity
+
+F32 = mybir.dt.float32
+BF16 = mybir.dt.bfloat16
+U32 = mybir.dt.uint32
+U8 = mybir.dt.uint8
+FP8X4 = mybir.dt.float8_e4m3fn_x4
+ALU = mybir.AluOpType
+ACT = mybir.ActivationFunctionType
+
+P = 128
+TOK = 4096
+D = 512
+F = 128
+NT = TOK // P
+EPS = 1e-5
+
+FLOPS = 2 * TOK * D * D + 2 * TOK * D * F
+
+SIZES = (2, 4, 4, 4, 4, 4, 4, 4, 2)
+MANUAL = True
+CA_AHEAD = 3
+XB_AHEAD = 2
+
+
+def tile_transformerblock_pb_t_kernel(tc, attn, x, w_out, b_out, ln2_g, ln2_b, w1, b1, out_0, out_1):
+    nc = tc.nc
+    attn_v = attn.flatten_outer_dims().rearrange("(p n) k -> p n k", n=NT)
+    x_v = x.flatten_outer_dims().rearrange("(p n) k -> p n k", n=NT)
+    xmid_v = out_0.flatten_outer_dims().rearrange("(p n) k -> p n k", n=NT)
+    hid_v = out_1.flatten_outer_dims().rearrange("(p n) k -> p n k", n=NT)
+    n_units = len(SIZES)
+    first = [sum(SIZES[:u]) for u in range(n_units)]
+    assert sum(SIZES) == NT
+
+    with ExitStack() as ctx:
+        const = ctx.enter_context(tc.tile_pool(name="const", bufs=1))
+        inp = ctx.enter_context(tc.tile_pool(name="inp", bufs=1))
+        work = ctx.enter_context(tc.tile_pool(name="work", bufs=2))
+        psum = ctx.enter_context(tc.psum_pool(name="psum", bufs=2))
+        if MANUAL:
+            ctx.enter_context(tc.manual_schedule())
+
+        T = {}
+
+        def ok(u):
+            return 0 <= u < n_units
+
+        ident_f = const.tile([P, P], F32)
+        make_identity(nc, ident_f[:])
+        ident_b = const.tile([P, P], BF16)
+        make_identity(nc, ident_b[:])
+
+        crow = const.tile([P, 2 * D], BF16)
+        nc.vector.memset(crow[:], 0.0)
+        grow = const.tile([P, P], BF16)
+        nc.vector.memset(grow[:], 0.0)
+        ones = const.tile([P, P], BF16)
+        nc.vector.memset(ones[:], 1.0)
+        neghalf = const.tile([P, 4], F32)
+        nc.vector.memset(neghalf[:], -0.5)
+        warm = const.tile([P, 2], F32)
+        nc.vector.memset(warm[:], 0.0)
+        nc.scalar.dma_start(out=crow[0:1, 0:D], in_=b_out.unsqueeze(0))
+        w1_raw = const.tile([P, 4, F], BF16)
+        for t in range(4):
+            nc.scalar.dma_start(out=w1_raw[:, t, :], in_=w1.rearrange("(g t i) f -> t g i f", t=4, i=8)[t])
+        nc.scalar.dma_start(out=crow[0:1, D:D + F], in_=b1.unsqueeze(0))
+        nc.scalar.dma_start(out=grow[0:4, :], in_=ln2_g.rearrange("(g t i) -> t g i", t=4, i=8))
+        nc.scalar.dma_start(out=grow[4:8, :], in_=ln2_b.rearrange("(g t i) -> t g i", t=4, i=8))
+        nc.scalar.activation(out=warm[:, 1:2], in_=warm[:, 0:1], func=ACT.Gelu)
+
+        w_raw = const.tile([P, 4, D], BF16)
+        for u in range(n_units):
+            n = SIZES[u]
+            a_t = inp.tile([P, n, D], BF16, name="attn%d" % u)
+            nc.sync.dma_start(out=a_t[:], in_=attn_v[:, first[u]:first[u] + n, :])
+            T["attn", u] = a_t
+            if u == 0:
+                nc.sync.dma_start(out=w_raw[:], in_=w_out.rearrange("(p t) d -> p t d", t=4))
+            x_t = inp.tile([P, n, D], BF16, name="x%d" % u)
+            nc.sync.dma_start(out=x_t[:], in_=x_v[:, first[u]:first[u] + n, :])
+            T["x", u] = x_t
+
+        w_grp = const.tile([P, D, 4], BF16, align_bytes=64)
+        w_codes = const.tile([P, D], U32, align_bytes=64)
+        w_scl = const.tile([P, D], U8, align_bytes=64)
+        w1_grp = const.tile([P, F, 4], BF16, align_bytes=64)
+        w1_codes = const.tile([P, F], U32, align_bytes=64)
+        w1_scl = const.tile([P, F], U8, align_bytes=64)
+        bo_sb = const.tile([P, D], F32)
+        b1_sb = const.tile([P, 4, F], F32)
+        gb = const.tile([P, 8], F32)
+
+        bo_ps = psum.tile([P, D], F32, tag="mm1", bufs=4)
+        nc.tensor.matmul(out=bo_ps[:], lhsT=ones[:], rhs=crow[:, 0:D], start=True, stop=True)
+        nc.scalar.copy(out=bo_sb[:], in_=bo_ps[:])
+        nc.vector.tensor_copy(out=w1_grp[:], in_=w1_raw[:].rearrange("q t f -> q f t"))
+        nc.vector.tensor_copy(out=w_grp[:].rearrange("q (c i) t -> q c t i", i=4),
+                              in_=w_raw[:].rearrange("q t (c i) -> q c t i", i=4))
+        nc.vector.quantize_mx(out=w1_codes[:].bitcast(FP8X4), scales=w1_scl[:],
+                              in_=w1_grp[:].rearrange("q f t -> q (f t)"))
+        nc.vector.quantize_mx(out=w_codes[:].bitcast(FP8X4), scales=w_scl[:],
+                              in_=w_grp[:].rearrange("q d t -> q (d t)"))
+
+        def consts_stage2():
+            b1_ps = psum.tile([P, D], F32, tag="mm1", bufs=4)
+            nc.tensor.matmul(out=b1_ps[:], lhsT=ones[:], rhs=crow[:, D:2 * D], start=True, stop=True)
+            gb_ps = psum.tile([P, P], BF16, tag="mm2", bufs=1)
+            nc.tensor.transpose(gb_ps[:], grow[:], ident_b[:])
+            nc.scalar.copy(out=b1_sb[:], in_=b1_ps[:, 0:F].unsqueeze(1).to_broadcast([P, 4, F]))
+            nc.scalar.copy(out=gb[:], in_=gb_ps[:, 0:8])
+
+        def st_ta(u):
+            n = SIZES[u]
+            banks = []
+            for h in range((n + 1) // 2):
+                m = min(2, n - 2 * h)
+                tpa = psum.tile([P, D], F32, tag="tp", bufs=3)
+                for jj in range(m):
+                    words = T["attn", u][:, 2 * h + jj, :].bitcast(F32)
+                    for uu in range(2):
+                        c0 = (2 * jj + uu) * P
+                        nc.tensor.transpose(tpa[:, c0:c0 + P], words[:, uu:2 * P:2], ident_f[:])
+                banks.append(tpa)
+            T["tpa", u] = banks
+
+        def st_ca(u):
+            n = SIZES[u]
+            grp1 = work.tile([P, n * P * 4], BF16, align_bytes=64, tag="grp1", bufs=3)
+            T["grp1", u] = grp1
+            g1f = grp1[:].bitcast(F32).rearrange("q (j r u) -> q j r u", j=n, u=2)
+            for h in range((n + 1) // 2):
+                m = min(2, n - 2 * h)
+                nc.scalar.copy(out=g1f[:, 2 * h:2 * h + m, :, :],
+                               in_=T["tpa", u][h][:, 0:m * 2 * P].rearrange("q (j u r) -> q j r u", j=m, u=2))
+
+        def st_q1(u):
+            n = SIZES[u]
+            a_codes = work.tile([P, n * P], U32, align_bytes=64, tag="a_codes", bufs=3)
+            a_scl = work.tile([P, n * P], U8, align_bytes=64, tag="a_scl", bufs=3)
+            nc.vector.quantize_mx(out=a_codes[:].bitcast(FP8X4), scales=a_scl[:], in_=T["grp1", u][:])
+            T["a_codes", u] = a_codes
+            T["a_scl", u] = a_scl
+
+        def st_xm(u):
+            T["xm", u] = work.tile([P, SIZES[u], D], F32, tag="xm", bufs=5, name="xm")
+
+        def st_xb(u, j, eng):
+            eng.tensor_tensor(out=T["xm", u][:, j, :], in0=T["x", u][:, j, :], in1=bo_sb[:], op=ALU.add)
+
+        def st_m1(u, j):
+            mm1 = psum.tile([P, D], F32, tag="mm1", bufs=4)
+            nc.tensor.matmul_mx(out=mm1[:], lhsT=T["a_codes", u][:, j * P:(j + 1) * P].bitcast(FP8X4),
+                                lhsT_scale=T["a_scl", u][:, j * P:(j + 1) * P],
+                                rhs=w_codes[:].bitcast(FP8X4), rhs_scale=w_scl[:], start=True, stop=True)
+            T["mm1", u, j] = mm1
+
+        def st_a(u, j):
+            if j == 0:
+                T["sums", u] = work.tile([P, 4], F32, tag="sums", bufs=4, name="sums")
+            xm = T["xm", u]
+            nc.vector.scalar_tensor_tensor(out=xm[:, j, :], in0=T["mm1", u, j][:], scalar=0.0, in1=xm[:, j, :],
+                                           op0=ALU.add, op1=ALU.add, accum_out=T["sums", u][:, j:j + 1])
+
+        def st_nm(u):
+            n = SIZES[u]
+            negmean = work.tile([P, 4], F32, tag="negmean", bufs=4)
+            nc.vector.tensor_scalar_mul(out=negmean[:, 0:n], in0=T["sums", u][:, 0:n], scalar1=-1.0 / D)
+            T["negmean", u] = negmean
+            nc.sync.dma_start(out=xmid_v[:, first[u]:first[u] + n, :], in_=T["xm", u][:])
+
+        def st_b(u):
+            ssq = work.tile([P, 4], F32, tag="ssq", bufs=4)
+            T["ssq", u] = ssq
+            for j in range(SIZES[u]):
+                junk = work.tile([P, D], BF16, tag="junk", bufs=2)
+                nc.scalar.activation(out=junk[:], in_=T["xm", u][:, j, :], func=ACT.Square,
+                                     bias=T["negmean", u][:, j:j + 1], scale=1.0, accum_out=ssq[:, j:j + 1])
+
+        def st_pow(u):
+            n = SIZES[u]
+            var = work.tile([P, 4], F32, tag="var", bufs=4)
+            nc.gpsimd.tensor_scalar(out=var[:, 0:n], in0=T["ssq", u][:, 0:n], scalar1=1.0 / D, scalar2=EPS,
+                                    op0=ALU.mult, op1=ALU.add)
+            rstd = work.tile([P, 4], F32, tag="rstd", bufs=4)
+            nc.gpsimd.tensor_tensor(out=rstd[:, 0:n], in0=var[:, 0:n], in1=neghalf[:, 0:n], op=ALU.pow)
+            T["rstd", u] = rstd
+
+        def st_c(u):
+            n = SIZES[u]
+            z = work.tile([P, n, D], F32, tag="z", bufs=2)
+            T["z", u] = z
+            for j in range(n):
+                nc.vector.tensor_scalar(out=z[:, j, :].rearrange("p (t g i) -> p t g i", t=4, i=8),
+                                        in0=T["xm", u][:, j, :].rearrange("p (g t i) -> p t g i", t=4, i=8), scalar1=T["negmean", u][:, j:j + 1],
+                                        scalar2=T["rstd", u][:, j:j + 1], op0=ALU.add, op1=ALU.mult)
+
+        def st_tz_d(u):
+            n = SIZES[u]
+            per_bank = 4 // n
+            planes = work.tile([P, 4, n * P], BF16, tag="planes", bufs=2)
+            T["planes", u] = planes
+            zt = None
+            for t in range(4):
+                if t % per_bank == 0:
+                    zt = psum.tile([P, D], F32, tag="tp", bufs=3)
+                c0 = (t % per_bank) * n * P
+                for j in range(n):
+                    nc.tensor.transpose(zt[:, c0 + j * P:c0 + (j + 1) * P], T["z", u][:, j, t * P:(t + 1) * P],
+                                        ident_f[:])
+                nc.scalar.activation(out=planes[:, t, :], in_=zt[:, c0:c0 + n * P], func=ACT.Identity,
+                                     bias=gb[:, 4 + t:5 + t], scale=gb[:, t:t + 1])
+
+        def st_r(u):
+            n = SIZES[u]
+            grp2 = work.tile([P, n * P, 4], BF16, align_bytes=64, tag="grp2", bufs=2)
+            T["grp2", u] = grp2
+            nc.vector.tensor_copy(out=grp2[:].rearrange("p (c i) t -> p c t i", i=4),
+                                  in_=T["planes", u][:].rearrange("p t (c i) -> p c t i", i=4))
+
+        def st_q2(u):
+            n = SIZES[u]
+            h_codes = work.tile([P, n * P], U32, align_bytes=64, tag="h_codes", bufs=2)
+            h_scl = work.tile([P, n * P], U8, align_bytes=64, tag="h_scl", bufs=2)
+            nc.vector.quantize_mx(out=h_codes[:].bitcast(FP8X4), scales=h_scl[:],
+                                  in_=T["grp2", u][:].rearrange("p r t -> p (r t)"))
+            T["h_codes", u] = h_codes
+            T["h_scl", u] = h_scl
+
+        def st_m2(u):
+            n = SIZES[u]
+            mm2 = psum.tile([P, n, F], F32, tag="mm2", bufs=1)
+            T["mm2", u] = mm2
+            for j in range(n):
+                nc.tensor.matmul_mx(out=mm2[:, j, :], lhsT=T["h_codes", u][:, j * P:(j + 1) * P].bitcast(FP8X4),
+                                    lhsT_scale=T["h_scl", u][:, j * P:(j + 1) * P],
+                                    rhs=w1_codes[:].bitcast(FP8X4), rhs_scale=w1_scl[:], start=True, stop=True)
+
+        def st_e(u):
+            n = SIZES[u]
+            pre = work.tile([P, n, F], F32, tag="pre", bufs=2)
+            nc.vector.tensor_tensor(out=pre[:], in0=T["mm2", u][:], in1=b1_sb[:, 0:n, :], op=ALU.add)
+            hid = work.tile([P, n, F], F32, tag="hid", bufs=3)
+            nc.scalar.activation(out=hid[:], in_=pre[:], func=ACT.Gelu)
+            nc.sync.dma_start(out=hid_v[:, first[u]:first[u] + n, :], in_=hid[:])
+
+        for s in range(-CA_AHEAD, n_units + 4):
+            if ok(s - 1):
+                st_pow(s - 1)
+            if ok(s + XB_AHEAD):
+                st_xm(s + XB_AHEAD)
+                for j in range(SIZES[s + XB_AHEAD] - 1):
+                    st_xb(s + XB_AHEAD, j, nc.gpsimd)
+            nxt = SIZES[s + 1] if ok(s + 1) else 0
+            issued = 0
+            if nxt and not ok(s):
+                st_q1(s + 1)
+            if ok(s):
+                n = SIZES[s]
+                for j in range(n):
+                    if j == n - 1:
+                        st_xb(s, j, nc.vector)
+                    st_a(s, j)
+                    if j == 0 and nxt:
+                        st_q1(s + 1)
+                    while issued < nxt and issued * n < (j + 1) * nxt:
+                        st_m1(s + 1, issued)
+                        issued += 1
+                st_nm(s)
+            while issued < nxt:
+                st_m1(s + 1, issued)
+                issued += 1
+            if ok(s):
+                st_b(s)
+            if ok(s - 1):
+                st_c(s - 1)
+                st_tz_d(s - 1)
+            if ok(s + CA_AHEAD):
+                st_ta(s + CA_AHEAD)
+            if s == -2:
+                consts_stage2()
+            if ok(s - 2):
+                st_r(s - 2)
+            if ok(s - 3):
+                st_e(s - 3)
+            if ok(s - 2):
+                st_q2(s - 2)
+                st_m2(s - 2)
+            if ok(s + CA_AHEAD):
+                st_ca(s + CA_AHEAD)

@@ -10,20 +10,23 @@ U8 = mybir.dt.uint8
 FP8X4 = mybir.dt.float8_e4m3fn_x4
 ALU = mybir.AluOpType
 ACT = mybir.ActivationFunctionType
-
 P = 128
 TOK = 4096
 D = 512
 F = 128
 NT = TOK // P
 EPS = 1e-5
-
 FLOPS = 2 * TOK * D * D + 2 * TOK * D * F
-
 SIZES = (2, 4, 4, 4, 4, 4, 4, 4, 2)
-MANUAL = True
 CA_AHEAD = 3
 XB_AHEAD = 2
+ZENG = "GGGG"
+XENG = "VVVV"
+BPS = True
+MM1 = 3
+TP = 3
+SUMB = False
+ORDER = ("pow", "z", "xb", "am", "nm", "e", "sq", "tz", "ta", "r", "q1b", "q2", "m2", "ca", "gl")
 
 
 def tile_transformerblock_pb_t_kernel(tc, attn, x, w_out, b_out, ln2_g, ln2_b, w1, b1, out_0, out_1):
@@ -34,16 +37,12 @@ def tile_transformerblock_pb_t_kernel(tc, attn, x, w_out, b_out, ln2_g, ln2_b, w
     hid_v = out_1.flatten_outer_dims().rearrange("(p n) k -> p n k", n=NT)
     n_units = len(SIZES)
     first = [sum(SIZES[:u]) for u in range(n_units)]
-    assert sum(SIZES) == NT
-
     with ExitStack() as ctx:
         const = ctx.enter_context(tc.tile_pool(name="const", bufs=1))
         inp = ctx.enter_context(tc.tile_pool(name="inp", bufs=1))
         work = ctx.enter_context(tc.tile_pool(name="work", bufs=2))
         psum = ctx.enter_context(tc.psum_pool(name="psum", bufs=2))
-        if MANUAL:
-            ctx.enter_context(tc.manual_schedule())
-
+        ctx.enter_context(tc.manual_schedule())
         T = {}
 
         def ok(u):
@@ -53,7 +52,6 @@ def tile_transformerblock_pb_t_kernel(tc, attn, x, w_out, b_out, ln2_g, ln2_b, w
         make_identity(nc, ident_f[:])
         ident_b = const.tile([P, P], BF16)
         make_identity(nc, ident_b[:])
-
         crow = const.tile([P, 2 * D], BF16)
         nc.vector.memset(crow[:], 0.0)
         grow = const.tile([P, P], BF16)
@@ -66,11 +64,6 @@ def tile_transformerblock_pb_t_kernel(tc, attn, x, w_out, b_out, ln2_g, ln2_b, w
         nc.vector.memset(warm[:], 0.0)
         nc.scalar.dma_start(out=crow[0:1, 0:D], in_=b_out.unsqueeze(0))
         w1_raw = const.tile([P, 4, F], BF16)
-        for t in range(4):
-            nc.scalar.dma_start(out=w1_raw[:, t, :], in_=w1.rearrange("(g t i) f -> t g i f", t=4, i=8)[t])
-        nc.scalar.dma_start(out=crow[0:1, D:D + F], in_=b1.unsqueeze(0))
-        nc.scalar.dma_start(out=grow[0:4, :], in_=ln2_g.rearrange("(g t i) -> t g i", t=4, i=8))
-        nc.scalar.dma_start(out=grow[4:8, :], in_=ln2_b.rearrange("(g t i) -> t g i", t=4, i=8))
         nc.scalar.activation(out=warm[:, 1:2], in_=warm[:, 0:1], func=ACT.Gelu)
 
         w_raw = const.tile([P, 4, D], BF16)
@@ -84,6 +77,12 @@ def tile_transformerblock_pb_t_kernel(tc, attn, x, w_out, b_out, ln2_g, ln2_b, w
             x_t = inp.tile([P, n, D], BF16, name="x%d" % u)
             nc.sync.dma_start(out=x_t[:], in_=x_v[:, first[u]:first[u] + n, :])
             T["x", u] = x_t
+            if u == 0:
+                for t in range(4):
+                    nc.sync.dma_start(out=w1_raw[:, t, :], in_=w1.rearrange("(g t i) f -> t g i f", t=4, i=8)[t])
+                nc.sync.dma_start(out=crow[0:1, D:D + F], in_=b1.unsqueeze(0))
+                nc.sync.dma_start(out=grow[0:4, :], in_=ln2_g.rearrange("(g t i) -> t g i", t=4, i=8))
+                nc.sync.dma_start(out=grow[4:8, :], in_=ln2_b.rearrange("(g t i) -> t g i", t=4, i=8))
 
         w_grp = const.tile([P, D, 4], BF16, align_bytes=64)
         w_codes = const.tile([P, D], U32, align_bytes=64)
@@ -91,35 +90,39 @@ def tile_transformerblock_pb_t_kernel(tc, attn, x, w_out, b_out, ln2_g, ln2_b, w
         w1_grp = const.tile([P, F, 4], BF16, align_bytes=64)
         w1_codes = const.tile([P, F], U32, align_bytes=64)
         w1_scl = const.tile([P, F], U8, align_bytes=64)
-        bo_sb = const.tile([P, D], F32)
         b1_sb = const.tile([P, 4, F], F32)
         gb = const.tile([P, 8], F32)
 
-        bo_ps = psum.tile([P, D], F32, tag="mm1", bufs=4)
-        nc.tensor.matmul(out=bo_ps[:], lhsT=ones[:], rhs=crow[:, 0:D], start=True, stop=True)
-        nc.scalar.copy(out=bo_sb[:], in_=bo_ps[:])
-        nc.vector.tensor_copy(out=w1_grp[:], in_=w1_raw[:].rearrange("q t f -> q f t"))
+        if BPS:
+            bo = psum.tile([P, D], F32, tag="bo", bufs=1)
+            nc.tensor.matmul(out=bo[:], lhsT=ones[:], rhs=crow[:, 0:D], start=True, stop=True)
+        else:
+            bo_ps = psum.tile([P, D], F32, tag="mm1", bufs=MM1)
+            nc.tensor.matmul(out=bo_ps[:], lhsT=ones[:], rhs=crow[:, 0:D], start=True, stop=True)
+            bo = const.tile([P, D], F32, name="bo")
+            nc.scalar.copy(out=bo[:], in_=bo_ps[:])
         nc.vector.tensor_copy(out=w_grp[:].rearrange("q (c i) t -> q c t i", i=4),
                               in_=w_raw[:].rearrange("q t (c i) -> q c t i", i=4))
-        nc.vector.quantize_mx(out=w1_codes[:].bitcast(FP8X4), scales=w1_scl[:],
-                              in_=w1_grp[:].rearrange("q f t -> q (f t)"))
         nc.vector.quantize_mx(out=w_codes[:].bitcast(FP8X4), scales=w_scl[:],
                               in_=w_grp[:].rearrange("q d t -> q (d t)"))
 
         def consts_stage2():
-            b1_ps = psum.tile([P, D], F32, tag="mm1", bufs=4)
+            b1_ps = psum.tile([P, D], F32, tag="mm1", bufs=MM1)
             nc.tensor.matmul(out=b1_ps[:], lhsT=ones[:], rhs=crow[:, D:2 * D], start=True, stop=True)
             gb_ps = psum.tile([P, P], BF16, tag="mm2", bufs=1)
             nc.tensor.transpose(gb_ps[:], grow[:], ident_b[:])
             nc.scalar.copy(out=b1_sb[:], in_=b1_ps[:, 0:F].unsqueeze(1).to_broadcast([P, 4, F]))
             nc.scalar.copy(out=gb[:], in_=gb_ps[:, 0:8])
+            nc.vector.tensor_copy(out=w1_grp[:], in_=w1_raw[:].rearrange("q t f -> q f t"))
+            nc.vector.quantize_mx(out=w1_codes[:].bitcast(FP8X4), scales=w1_scl[:],
+                                  in_=w1_grp[:].rearrange("q f t -> q (f t)"))
 
         def st_ta(u):
             n = SIZES[u]
             banks = []
             for h in range((n + 1) // 2):
                 m = min(2, n - 2 * h)
-                tpa = psum.tile([P, D], F32, tag="tp", bufs=3)
+                tpa = psum.tile([P, D], F32, tag="tp", bufs=TP)
                 for jj in range(m):
                     words = T["attn", u][:, 2 * h + jj, :].bitcast(F32)
                     for uu in range(2):
@@ -146,14 +149,19 @@ def tile_transformerblock_pb_t_kernel(tc, attn, x, w_out, b_out, ln2_g, ln2_b, w
             T["a_codes", u] = a_codes
             T["a_scl", u] = a_scl
 
-        def st_xm(u):
-            T["xm", u] = work.tile([P, SIZES[u], D], F32, tag="xm", bufs=5, name="xm")
-
-        def st_xb(u, j, eng):
-            eng.tensor_tensor(out=T["xm", u][:, j, :], in0=T["x", u][:, j, :], in1=bo_sb[:], op=ALU.add)
+        def st_xb(u):
+            n = SIZES[u]
+            xm = work.tile([P, n, D], F32, tag="xm", bufs=5, name="xm")
+            T["xm", u] = xm
+            e = XENG[4 - n:]
+            for j in range(n):
+                if e[j] == "G":
+                    nc.gpsimd.tensor_tensor(out=xm[:, j, :], in0=T["x", u][:, j, :], in1=bo[:], op=ALU.add)
+                else:
+                    nc.vector.tensor_tensor(out=xm[:, j, :], in0=bo[:], in1=T["x", u][:, j, :], op=ALU.add)
 
         def st_m1(u, j):
-            mm1 = psum.tile([P, D], F32, tag="mm1", bufs=4)
+            mm1 = psum.tile([P, D], F32, tag="mm1", bufs=MM1)
             nc.tensor.matmul_mx(out=mm1[:], lhsT=T["a_codes", u][:, j * P:(j + 1) * P].bitcast(FP8X4),
                                 lhsT_scale=T["a_scl", u][:, j * P:(j + 1) * P],
                                 rhs=w_codes[:].bitcast(FP8X4), rhs_scale=w_scl[:], start=True, stop=True)
@@ -166,6 +174,20 @@ def tile_transformerblock_pb_t_kernel(tc, attn, x, w_out, b_out, ln2_g, ln2_b, w
             nc.vector.scalar_tensor_tensor(out=xm[:, j, :], in0=T["mm1", u, j][:], scalar=0.0, in1=xm[:, j, :],
                                            op0=ALU.add, op1=ALU.add, accum_out=T["sums", u][:, j:j + 1])
 
+        def st_am(s):
+            nxt = SIZES[s + 1] if ok(s + 1) else 0
+            issued = 0
+            if ok(s):
+                n = SIZES[s]
+                for j in range(n):
+                    st_a(s, j)
+                    while issued < nxt and issued * n < (j + 1) * nxt:
+                        st_m1(s + 1, issued)
+                        issued += 1
+            while issued < nxt:
+                st_m1(s + 1, issued)
+                issued += 1
+
         def st_nm(u):
             n = SIZES[u]
             negmean = work.tile([P, 4], F32, tag="negmean", bufs=4)
@@ -173,7 +195,7 @@ def tile_transformerblock_pb_t_kernel(tc, attn, x, w_out, b_out, ln2_g, ln2_b, w
             T["negmean", u] = negmean
             nc.sync.dma_start(out=xmid_v[:, first[u]:first[u] + n, :], in_=T["xm", u][:])
 
-        def st_b(u):
+        def st_sq(u):
             ssq = work.tile([P, 4], F32, tag="ssq", bufs=4)
             T["ssq", u] = ssq
             for j in range(SIZES[u]):
@@ -190,16 +212,18 @@ def tile_transformerblock_pb_t_kernel(tc, attn, x, w_out, b_out, ln2_g, ln2_b, w
             nc.gpsimd.tensor_tensor(out=rstd[:, 0:n], in0=var[:, 0:n], in1=neghalf[:, 0:n], op=ALU.pow)
             T["rstd", u] = rstd
 
-        def st_c(u):
+        def st_z(u):
             n = SIZES[u]
             z = work.tile([P, n, D], F32, tag="z", bufs=2)
             T["z", u] = z
             for j in range(n):
-                nc.vector.tensor_scalar(out=z[:, j, :].rearrange("p (t g i) -> p t g i", t=4, i=8),
-                                        in0=T["xm", u][:, j, :].rearrange("p (g t i) -> p t g i", t=4, i=8), scalar1=T["negmean", u][:, j:j + 1],
-                                        scalar2=T["rstd", u][:, j:j + 1], op0=ALU.add, op1=ALU.mult)
+                eng = nc.gpsimd if ZENG[4 - n:][j] == "G" else nc.vector
+                eng.tensor_scalar(out=z[:, j, :].rearrange("p (t g i) -> p t g i", t=4, i=8),
+                                  in0=T["xm", u][:, j, :].rearrange("p (g t i) -> p t g i", t=4, i=8),
+                                  scalar1=T["negmean", u][:, j:j + 1],
+                                  scalar2=T["rstd", u][:, j:j + 1], op0=ALU.add, op1=ALU.mult)
 
-        def st_tz_d(u):
+        def st_tz(u):
             n = SIZES[u]
             per_bank = 4 // n
             planes = work.tile([P, 4, n * P], BF16, tag="planes", bufs=2)
@@ -207,7 +231,7 @@ def tile_transformerblock_pb_t_kernel(tc, attn, x, w_out, b_out, ln2_g, ln2_b, w
             zt = None
             for t in range(4):
                 if t % per_bank == 0:
-                    zt = psum.tile([P, D], F32, tag="tp", bufs=3)
+                    zt = psum.tile([P, D], F32, tag="tp", bufs=TP)
                 c0 = (t % per_bank) * n * P
                 for j in range(n):
                     nc.tensor.transpose(zt[:, c0 + j * P:c0 + (j + 1) * P], T["z", u][:, j, t * P:(t + 1) * P],
@@ -244,51 +268,26 @@ def tile_transformerblock_pb_t_kernel(tc, attn, x, w_out, b_out, ln2_g, ln2_b, w
             n = SIZES[u]
             pre = work.tile([P, n, F], F32, tag="pre", bufs=2)
             nc.vector.tensor_tensor(out=pre[:], in0=T["mm2", u][:], in1=b1_sb[:, 0:n, :], op=ALU.add)
+            T["pre", u] = pre
+
+        def st_gl(u):
+            n = SIZES[u]
             hid = work.tile([P, n, F], F32, tag="hid", bufs=3)
-            nc.scalar.activation(out=hid[:], in_=pre[:], func=ACT.Gelu)
+            nc.scalar.activation(out=hid[:], in_=T["pre", u][:], func=ACT.Gelu)
             nc.sync.dma_start(out=hid_v[:, first[u]:first[u] + n, :], in_=hid[:])
 
+        fns = {"pow": (st_pow, -1), "z": (st_z, -1), "xb": (st_xb, XB_AHEAD), "nm": (st_nm, 0), "e": (st_e, -3),
+               "sq": (st_sq, 0), "tz": (st_tz, -1), "ta": (st_ta, CA_AHEAD), "r": (st_r, -2), "q1": (st_q1, 1), "q1b": (st_q1, 2),
+               "q2": (st_q2, -2), "m2": (st_m2, -2), "ca": (st_ca, CA_AHEAD), "gl": (st_gl, -3), "xb1": (st_xb, 1), "z0": (st_z, 0), "pow0": (st_pow, 0), "tz0": (st_tz, 0),
+               "r1": (st_r, -1), "q21": (st_q2, -1), "m21": (st_m2, -1), "e2": (st_e, -2), "gl2": (st_gl, -2), "e1": (st_e, -1), "gl1": (st_gl, -1), "ca2": (st_ca, 2), "ta2": (st_ta, 2)}
         for s in range(-CA_AHEAD, n_units + 4):
-            if ok(s - 1):
-                st_pow(s - 1)
-            if ok(s + XB_AHEAD):
-                st_xm(s + XB_AHEAD)
-                for j in range(SIZES[s + XB_AHEAD] - 1):
-                    st_xb(s + XB_AHEAD, j, nc.gpsimd)
-            nxt = SIZES[s + 1] if ok(s + 1) else 0
-            issued = 0
-            if nxt and not ok(s):
-                st_q1(s + 1)
-            if ok(s):
-                n = SIZES[s]
-                for j in range(n):
-                    if j == n - 1:
-                        st_xb(s, j, nc.vector)
-                    st_a(s, j)
-                    if j == 0 and nxt:
-                        st_q1(s + 1)
-                    while issued < nxt and issued * n < (j + 1) * nxt:
-                        st_m1(s + 1, issued)
-                        issued += 1
-                st_nm(s)
-            while issued < nxt:
-                st_m1(s + 1, issued)
-                issued += 1
-            if ok(s):
-                st_b(s)
-            if ok(s - 1):
-                st_c(s - 1)
-                st_tz_d(s - 1)
-            if ok(s + CA_AHEAD):
-                st_ta(s + CA_AHEAD)
+            for name in ORDER:
+                if name == "am":
+                    if s >= -1:
+                        st_am(s)
+                else:
+                    f, o = fns[name]
+                    if ok(s + o):
+                        f(s + o)
             if s == -2:
                 consts_stage2()
-            if ok(s - 2):
-                st_r(s - 2)
-            if ok(s - 3):
-                st_e(s - 3)
-            if ok(s - 2):
-                st_q2(s - 2)
-                st_m2(s - 2)
-            if ok(s + CA_AHEAD):
-                st_ca(s + CA_AHEAD)

@@ -26,7 +26,7 @@ BPS = True
 MM1 = 3
 TP = 3
 SUMB = False
-ORDER = ("pow", "z", "xb", "am", "nm", "e", "sq", "tz", "ta", "r", "q1b", "q2", "m2", "ca", "gl")
+ORDER = ("pow", "z", "am", "e", "nm", "sq", "tz", "ta", "r", "q1b", "q2", "m2", "ca", "gl", "xb1")
 
 
 def tile_transformerblock_pb_t_kernel(tc, attn, x, w_out, b_out, ln2_g, ln2_b, w1, b1, out_0, out_1):
@@ -174,19 +174,23 @@ def tile_transformerblock_pb_t_kernel(tc, attn, x, w_out, b_out, ln2_g, ln2_b, w
             nc.vector.scalar_tensor_tensor(out=xm[:, j, :], in0=T["mm1", u, j][:], scalar=0.0, in1=xm[:, j, :],
                                            op0=ALU.add, op1=ALU.add, accum_out=T["sums", u][:, j:j + 1])
 
+        tiles = [(u, j) for u in range(n_units) for j in range(SIZES[u])]
+        m1_done = []
+
         def st_am(s):
-            nxt = SIZES[s + 1] if ok(s + 1) else 0
-            issued = 0
+            if s == -1:
+                while len(m1_done) < min(MM1, NT) and tiles[len(m1_done)][0] == 0:
+                    st_m1(*tiles[len(m1_done)])
+                    m1_done.append(1)
             if ok(s):
-                n = SIZES[s]
-                for j in range(n):
+                for j in range(SIZES[s]):
+                    while len(m1_done) < min(NT, first[s] + j + MM1) and tiles[len(m1_done)][0] <= s + 1:
+                        st_m1(*tiles[len(m1_done)])
+                        m1_done.append(1)
                     st_a(s, j)
-                    while issued < nxt and issued * n < (j + 1) * nxt:
-                        st_m1(s + 1, issued)
-                        issued += 1
-            while issued < nxt:
-                st_m1(s + 1, issued)
-                issued += 1
+                while len(m1_done) < min(NT, first[s] + SIZES[s] + MM1) and tiles[len(m1_done)][0] <= s + 1:
+                    st_m1(*tiles[len(m1_done)])
+                    m1_done.append(1)
 
         def st_nm(u):
             n = SIZES[u]
@@ -228,16 +232,16 @@ def tile_transformerblock_pb_t_kernel(tc, attn, x, w_out, b_out, ln2_g, ln2_b, w
             per_bank = 4 // n
             planes = work.tile([P, 4, n * P], BF16, tag="planes", bufs=2)
             T["planes", u] = planes
-            zt = None
-            for t in range(4):
-                if t % per_bank == 0:
-                    zt = psum.tile([P, D], F32, tag="tp", bufs=TP)
-                c0 = (t % per_bank) * n * P
-                for j in range(n):
-                    nc.tensor.transpose(zt[:, c0 + j * P:c0 + (j + 1) * P], T["z", u][:, j, t * P:(t + 1) * P],
-                                        ident_f[:])
-                nc.scalar.activation(out=planes[:, t, :], in_=zt[:, c0:c0 + n * P], func=ACT.Identity,
-                                     bias=gb[:, 4 + t:5 + t], scale=gb[:, t:t + 1])
+            for t0 in range(0, 4, per_bank):
+                zt = psum.tile([P, D], F32, tag="tp", bufs=TP)
+                for t in range(t0, t0 + per_bank):
+                    for j in range(n):
+                        c0 = ((t - t0) * n + j) * P
+                        nc.tensor.transpose(zt[:, c0:c0 + P], T["z", u][:, j, t * P:(t + 1) * P], ident_f[:])
+                for t in range(t0, t0 + per_bank):
+                    c0 = (t - t0) * n * P
+                    nc.scalar.activation(out=planes[:, t, :], in_=zt[:, c0:c0 + n * P], func=ACT.Identity,
+                                         bias=gb[:, 4 + t:5 + t], scale=gb[:, t:t + 1])
 
         def st_r(u):
             n = SIZES[u]

@@ -23,10 +23,16 @@ XB_AHEAD = 2
 ZENG = "GGGG"
 XENG = "VVVV"
 BPS = True
-MM1 = 3
+MM1 = 4
 TP = 3
-SUMB = False
-ORDER = ("pow", "z", "am", "e", "nm", "sq", "tz", "ta", "r", "q1b", "q2", "m2", "ca", "gl", "xb1")
+DUP = 0
+MM2 = "tp"
+ZLAST = 2
+NMENG = "V"
+CONST_AT = 2
+C2 = 0
+S0 = -4
+ORDER = "pow-1 z-1:0123 a+0:0 m1+1:0 a+0:1 m1+1:1 a+0:2 m1+1:2 a+0:3 m1+1:3 nm+0 sq+0:0123 tz-1:0 tz-1:1 tz-1:2 d-1:0 tz-1:3 d-1:123 ta+3:01 r-2 e-3 gl-3 q1+2 q2-2 m2-2 ca+3:01 xb+1:0123"
 
 
 def tile_transformerblock_pb_t_kernel(tc, attn, x, w_out, b_out, ln2_g, ln2_b, w1, b1, out_0, out_1):
@@ -77,7 +83,7 @@ def tile_transformerblock_pb_t_kernel(tc, attn, x, w_out, b_out, ln2_g, ln2_b, w
             x_t = inp.tile([P, n, D], BF16, name="x%d" % u)
             nc.sync.dma_start(out=x_t[:], in_=x_v[:, first[u]:first[u] + n, :])
             T["x", u] = x_t
-            if u == 0:
+            if u == CONST_AT:
                 for t in range(4):
                     nc.sync.dma_start(out=w1_raw[:, t, :], in_=w1.rearrange("(g t i) f -> t g i f", t=4, i=8)[t])
                 nc.sync.dma_start(out=crow[0:1, D:D + F], in_=b1.unsqueeze(0))
@@ -109,7 +115,7 @@ def tile_transformerblock_pb_t_kernel(tc, attn, x, w_out, b_out, ln2_g, ln2_b, w
         def consts_stage2():
             b1_ps = psum.tile([P, D], F32, tag="mm1", bufs=MM1)
             nc.tensor.matmul(out=b1_ps[:], lhsT=ones[:], rhs=crow[:, D:2 * D], start=True, stop=True)
-            gb_ps = psum.tile([P, P], BF16, tag="mm2", bufs=1)
+            gb_ps = psum.tile([P, P], BF16, tag=MM2, bufs=TP if MM2 == "tp" else 1)
             nc.tensor.transpose(gb_ps[:], grow[:], ident_b[:])
             nc.scalar.copy(out=b1_sb[:], in_=b1_ps[:, 0:F].unsqueeze(1).to_broadcast([P, 4, F]))
             nc.scalar.copy(out=gb[:], in_=gb_ps[:, 0:8])
@@ -117,29 +123,29 @@ def tile_transformerblock_pb_t_kernel(tc, attn, x, w_out, b_out, ln2_g, ln2_b, w
             nc.vector.quantize_mx(out=w1_codes[:].bitcast(FP8X4), scales=w1_scl[:],
                                   in_=w1_grp[:].rearrange("q f t -> q (f t)"))
 
-        def st_ta(u):
+        def st_ta(u, h):
             n = SIZES[u]
-            banks = []
-            for h in range((n + 1) // 2):
-                m = min(2, n - 2 * h)
-                tpa = psum.tile([P, D], F32, tag="tp", bufs=TP)
-                for jj in range(m):
-                    words = T["attn", u][:, 2 * h + jj, :].bitcast(F32)
-                    for uu in range(2):
-                        c0 = (2 * jj + uu) * P
-                        nc.tensor.transpose(tpa[:, c0:c0 + P], words[:, uu:2 * P:2], ident_f[:])
-                banks.append(tpa)
-            T["tpa", u] = banks
+            m = min(2, n - 2 * h)
+            if m <= 0:
+                return
+            tpa = psum.tile([P, D], F32, tag="tp", bufs=TP)
+            for jj in range(m):
+                words = T["attn", u][:, 2 * h + jj, :].bitcast(F32)
+                for uu in range(2):
+                    c0 = (2 * jj + uu) * P
+                    nc.tensor.transpose(tpa[:, c0:c0 + P], words[:, uu:2 * P:2], ident_f[:])
+            T["tpa", u, h] = tpa
 
-        def st_ca(u):
+        def st_ca(u, h):
             n = SIZES[u]
-            grp1 = work.tile([P, n * P * 4], BF16, align_bytes=64, tag="grp1", bufs=3)
-            T["grp1", u] = grp1
-            g1f = grp1[:].bitcast(F32).rearrange("q (j r u) -> q j r u", j=n, u=2)
-            for h in range((n + 1) // 2):
-                m = min(2, n - 2 * h)
-                nc.scalar.copy(out=g1f[:, 2 * h:2 * h + m, :, :],
-                               in_=T["tpa", u][h][:, 0:m * 2 * P].rearrange("q (j u r) -> q j r u", j=m, u=2))
+            m = min(2, n - 2 * h)
+            if h == 0:
+                T["grp1", u] = work.tile([P, n * P * 4], BF16, align_bytes=64, tag="grp1", bufs=3, name="grp1")
+            if m <= 0:
+                return
+            g1f = T["grp1", u][:].bitcast(F32).rearrange("q (j r u) -> q j r u", j=n, u=2)
+            nc.scalar.copy(out=g1f[:, 2 * h:2 * h + m, :, :],
+                           in_=T["tpa", u, h][:, 0:m * 2 * P].rearrange("q (j u r) -> q j r u", j=m, u=2))
 
         def st_q1(u):
             n = SIZES[u]
@@ -149,63 +155,55 @@ def tile_transformerblock_pb_t_kernel(tc, attn, x, w_out, b_out, ln2_g, ln2_b, w
             T["a_codes", u] = a_codes
             T["a_scl", u] = a_scl
 
-        def st_xb(u):
+        def st_xb(u, j):
             n = SIZES[u]
-            xm = work.tile([P, n, D], F32, tag="xm", bufs=5, name="xm")
-            T["xm", u] = xm
-            e = XENG[4 - n:]
-            for j in range(n):
-                if e[j] == "G":
-                    nc.gpsimd.tensor_tensor(out=xm[:, j, :], in0=T["x", u][:, j, :], in1=bo[:], op=ALU.add)
-                else:
-                    nc.vector.tensor_tensor(out=xm[:, j, :], in0=bo[:], in1=T["x", u][:, j, :], op=ALU.add)
+            if j == 0:
+                T["xm", u] = work.tile([P, n, D], F32, tag="xm", bufs=5, name="xm")
+            if j >= n:
+                return
+            xm = T["xm", u]
+            if XENG[j] == "G":
+                nc.gpsimd.tensor_tensor(out=xm[:, j, :], in0=T["x", u][:, j, :], in1=bo[:], op=ALU.add)
+            else:
+                nc.vector.tensor_tensor(out=xm[:, j, :], in0=bo[:], in1=T["x", u][:, j, :], op=ALU.add)
 
         def st_m1(u, j):
+            if j >= SIZES[u]:
+                return
             mm1 = psum.tile([P, D], F32, tag="mm1", bufs=MM1)
-            nc.tensor.matmul_mx(out=mm1[:], lhsT=T["a_codes", u][:, j * P:(j + 1) * P].bitcast(FP8X4),
+            for rep in range(1 + (DUP if isinstance(DUP, int) else DUP[j % len(DUP)])):
+                nc.tensor.matmul_mx(out=mm1[:], lhsT=T["a_codes", u][:, j * P:(j + 1) * P].bitcast(FP8X4),
                                 lhsT_scale=T["a_scl", u][:, j * P:(j + 1) * P],
                                 rhs=w_codes[:].bitcast(FP8X4), rhs_scale=w_scl[:], start=True, stop=True)
             T["mm1", u, j] = mm1
 
         def st_a(u, j):
+            if j >= SIZES[u]:
+                return
             if j == 0:
                 T["sums", u] = work.tile([P, 4], F32, tag="sums", bufs=4, name="sums")
             xm = T["xm", u]
             nc.vector.scalar_tensor_tensor(out=xm[:, j, :], in0=T["mm1", u, j][:], scalar=0.0, in1=xm[:, j, :],
                                            op0=ALU.add, op1=ALU.add, accum_out=T["sums", u][:, j:j + 1])
 
-        tiles = [(u, j) for u in range(n_units) for j in range(SIZES[u])]
-        m1_done = []
-
-        def st_am(s):
-            if s == -1:
-                while len(m1_done) < min(MM1, NT) and tiles[len(m1_done)][0] == 0:
-                    st_m1(*tiles[len(m1_done)])
-                    m1_done.append(1)
-            if ok(s):
-                for j in range(SIZES[s]):
-                    while len(m1_done) < min(NT, first[s] + j + MM1) and tiles[len(m1_done)][0] <= s + 1:
-                        st_m1(*tiles[len(m1_done)])
-                        m1_done.append(1)
-                    st_a(s, j)
-                while len(m1_done) < min(NT, first[s] + SIZES[s] + MM1) and tiles[len(m1_done)][0] <= s + 1:
-                    st_m1(*tiles[len(m1_done)])
-                    m1_done.append(1)
-
         def st_nm(u):
             n = SIZES[u]
             negmean = work.tile([P, 4], F32, tag="negmean", bufs=4)
-            nc.vector.tensor_scalar_mul(out=negmean[:, 0:n], in0=T["sums", u][:, 0:n], scalar1=-1.0 / D)
+            if NMENG == "V":
+                nc.vector.tensor_scalar_mul(out=negmean[:, 0:n], in0=T["sums", u][:, 0:n], scalar1=-1.0 / D)
+            else:
+                nc.gpsimd.tensor_scalar(out=negmean[:, 0:n], in0=T["sums", u][:, 0:n], scalar1=-1.0 / D, scalar2=0.0, op0=ALU.mult, op1=ALU.add)
             T["negmean", u] = negmean
             nc.sync.dma_start(out=xmid_v[:, first[u]:first[u] + n, :], in_=T["xm", u][:])
 
-        def st_sq(u):
-            ssq = work.tile([P, 4], F32, tag="ssq", bufs=4)
-            T["ssq", u] = ssq
-            for j in range(SIZES[u]):
-                junk = work.tile([P, D], BF16, tag="junk", bufs=2)
-                nc.scalar.activation(out=junk[:], in_=T["xm", u][:, j, :], func=ACT.Square,
-                                     bias=T["negmean", u][:, j:j + 1], scale=1.0, accum_out=ssq[:, j:j + 1])
+        def st_sq(u, j):
+            if j == 0:
+                T["ssq", u] = work.tile([P, 4], F32, tag="ssq", bufs=4, name="ssq")
+            if j >= SIZES[u]:
+                return
+            junk = work.tile([P, D], BF16, tag="junk", bufs=2)
+            nc.scalar.activation(out=junk[:], in_=T["xm", u][:, j, :], func=ACT.Square, bias=T["negmean", u][:, j:j + 1],
+                                 scale=1.0, accum_out=T["ssq", u][:, j:j + 1])
 
         def st_pow(u):
             n = SIZES[u]
@@ -215,33 +213,52 @@ def tile_transformerblock_pb_t_kernel(tc, attn, x, w_out, b_out, ln2_g, ln2_b, w
             rstd = work.tile([P, 4], F32, tag="rstd", bufs=4)
             nc.gpsimd.tensor_tensor(out=rstd[:, 0:n], in0=var[:, 0:n], in1=neghalf[:, 0:n], op=ALU.pow)
             T["rstd", u] = rstd
+            if "S" in ZENG:
+                nmr = work.tile([P, 4], F32, tag="nmr", bufs=4)
+                nc.gpsimd.tensor_tensor(out=nmr[:, 0:n], in0=T["negmean", u][:, 0:n], in1=rstd[:, 0:n], op=ALU.mult)
+                T["nmr", u] = nmr
 
-        def st_z(u):
+        def st_z(u, j):
             n = SIZES[u]
-            z = work.tile([P, n, D], F32, tag="z", bufs=2)
-            T["z", u] = z
-            for j in range(n):
-                eng = nc.gpsimd if ZENG[4 - n:][j] == "G" else nc.vector
-                eng.tensor_scalar(out=z[:, j, :].rearrange("p (t g i) -> p t g i", t=4, i=8),
-                                  in0=T["xm", u][:, j, :].rearrange("p (g t i) -> p t g i", t=4, i=8),
-                                  scalar1=T["negmean", u][:, j:j + 1],
+            if j == 0:
+                T["z", u] = work.tile([P, n, D], F32, tag="z", bufs=2, name="z")
+            if j >= n:
+                return
+            z = T["z", u]
+            k = "V" if u >= len(SIZES) - ZLAST else ZENG[j]
+            o = z[:, j, :].rearrange("p (t g i) -> p t g i", t=4, i=8)
+            xv = T["xm", u][:, j, :].rearrange("p (g t i) -> p t g i", t=4, i=8)
+            if k == "S":
+                nc.scalar.activation(out=o, in_=xv, func=ACT.Identity, bias=T["nmr", u][:, j:j + 1], scale=T["rstd", u][:, j:j + 1])
+            else:
+                eng = nc.gpsimd if k == "G" else nc.vector
+                eng.tensor_scalar(out=o, in0=xv, scalar1=T["negmean", u][:, j:j + 1],
                                   scalar2=T["rstd", u][:, j:j + 1], op0=ALU.add, op1=ALU.mult)
 
-        def st_tz(u):
+        def st_tz(u, t0):
             n = SIZES[u]
             per_bank = 4 // n
-            planes = work.tile([P, 4, n * P], BF16, tag="planes", bufs=2)
-            T["planes", u] = planes
-            for t0 in range(0, 4, per_bank):
-                zt = psum.tile([P, D], F32, tag="tp", bufs=TP)
-                for t in range(t0, t0 + per_bank):
-                    for j in range(n):
-                        c0 = ((t - t0) * n + j) * P
-                        nc.tensor.transpose(zt[:, c0:c0 + P], T["z", u][:, j, t * P:(t + 1) * P], ident_f[:])
-                for t in range(t0, t0 + per_bank):
-                    c0 = (t - t0) * n * P
-                    nc.scalar.activation(out=planes[:, t, :], in_=zt[:, c0:c0 + n * P], func=ACT.Identity,
-                                         bias=gb[:, 4 + t:5 + t], scale=gb[:, t:t + 1])
+            if t0 % per_bank:
+                return
+            if t0 == 0:
+                T["planes", u] = work.tile([P, 4, n * P], BF16, tag="planes", bufs=2, name="planes")
+            zt = psum.tile([P, D], F32, tag="tp", bufs=TP)
+            for t in range(t0, t0 + per_bank):
+                for j in range(n):
+                    c0 = ((t - t0) * n + j) * P
+                    nc.tensor.transpose(zt[:, c0:c0 + P], T["z", u][:, j, t * P:(t + 1) * P], ident_f[:])
+            T["zt", u, t0] = zt
+
+        def st_d(u, t0):
+            n = SIZES[u]
+            per_bank = 4 // n
+            if t0 % per_bank:
+                return
+            zt = T["zt", u, t0]
+            for t in range(t0, t0 + per_bank):
+                c0 = (t - t0) * n * P
+                nc.scalar.activation(out=T["planes", u][:, t, :], in_=zt[:, c0:c0 + n * P], func=ACT.Identity,
+                                     bias=gb[:, 4 + t:5 + t], scale=gb[:, t:t + 1])
 
         def st_r(u):
             n = SIZES[u]
@@ -261,7 +278,7 @@ def tile_transformerblock_pb_t_kernel(tc, attn, x, w_out, b_out, ln2_g, ln2_b, w
 
         def st_m2(u):
             n = SIZES[u]
-            mm2 = psum.tile([P, n, F], F32, tag="mm2", bufs=1)
+            mm2 = psum.tile([P, n, F], F32, name="mm2", tag=MM2, bufs=TP if MM2 == "tp" else 1)
             T["mm2", u] = mm2
             for j in range(n):
                 nc.tensor.matmul_mx(out=mm2[:, j, :], lhsT=T["h_codes", u][:, j * P:(j + 1) * P].bitcast(FP8X4),
@@ -280,18 +297,19 @@ def tile_transformerblock_pb_t_kernel(tc, attn, x, w_out, b_out, ln2_g, ln2_b, w
             nc.scalar.activation(out=hid[:], in_=T["pre", u][:], func=ACT.Gelu)
             nc.sync.dma_start(out=hid_v[:, first[u]:first[u] + n, :], in_=hid[:])
 
-        fns = {"pow": (st_pow, -1), "z": (st_z, -1), "xb": (st_xb, XB_AHEAD), "nm": (st_nm, 0), "e": (st_e, -3),
-               "sq": (st_sq, 0), "tz": (st_tz, -1), "ta": (st_ta, CA_AHEAD), "r": (st_r, -2), "q1": (st_q1, 1), "q1b": (st_q1, 2),
-               "q2": (st_q2, -2), "m2": (st_m2, -2), "ca": (st_ca, CA_AHEAD), "gl": (st_gl, -3), "xb1": (st_xb, 1), "z0": (st_z, 0), "pow0": (st_pow, 0), "tz0": (st_tz, 0),
-               "r1": (st_r, -1), "q21": (st_q2, -1), "m21": (st_m2, -1), "e2": (st_e, -2), "gl2": (st_gl, -2), "e1": (st_e, -1), "gl1": (st_gl, -1), "ca2": (st_ca, 2), "ta2": (st_ta, 2)}
-        for s in range(-CA_AHEAD, n_units + 4):
-            for name in ORDER:
-                if name == "am":
-                    if s >= -1:
-                        st_am(s)
-                else:
-                    f, o = fns[name]
-                    if ok(s + o):
-                        f(s + o)
-            if s == -2:
+        fns = {"pow": st_pow, "z": st_z, "xb": st_xb, "nm": st_nm, "e": st_e, "sq": st_sq, "tz": st_tz, "d": st_d,
+               "ta": st_ta, "r": st_r, "q1": st_q1, "q2": st_q2, "m2": st_m2, "ca": st_ca, "gl": st_gl, "a": st_a, "m1": st_m1}
+        steps = []
+        for tok in ORDER.split(" "):
+            body = tok.split(":")
+            k = body[0].replace("+", " ").replace("-", " -").split(" ")
+            steps.append((fns[k[0]], int(k[1]), [int(c) for c in body[1]] if len(body) > 1 else None))
+        for s in range(S0, n_units + 4):
+            if s == C2:
                 consts_stage2()
+            for f, o, js in steps:
+                if ok(s + o):
+                    if js is None:
+                        f(s + o)
+                    for j in js or []:
+                        f(s + o, j)

@@ -17,22 +17,36 @@ F = 128
 NT = TOK // P
 EPS = 1e-5
 FLOPS = 2 * TOK * D * D + 2 * TOK * D * F
-SIZES = (2, 4, 4, 4, 4, 4, 4, 4, 2)
+SIZES = (2, 2, 4, 4, 4, 4, 4, 4, 2, 2)
 CA_AHEAD = 3
 XB_AHEAD = 2
 ZENG = "GGGG"
-XENG = "VVVV"
+XMB = 5
 BPS = True
 MM1 = 4
 TP = 3
 DUP = 0
 MM2 = "tp"
-ZLAST = 2
+ZLAST = 3
 NMENG = "V"
 CONST_AT = 2
 C2 = 0
 S0 = -4
-ORDER = "pow-1 z-1:0123 a+0:0 m1+1:0 a+0:1 m1+1:1 a+0:2 m1+1:2 a+0:3 m1+1:3 nm+0 sq+0:0123 tz-1:0 tz-1:1 tz-1:2 d-1:0 tz-1:3 d-1:123 ta+3:01 r-2 e-3 gl-3 q1+2 q2-2 m2-2 ca+3:01 xb+1:0123"
+BO = -2
+WS = 0
+WFIRST = False
+RS = 0
+SUMB = True
+GX = 0
+NB = 4
+ZB = 2
+PB = 2
+AB = 3
+TAIL = 4
+E2 = False
+EVENG = "S"
+W1V = True
+ORDER = "pow-1 z-1:0123 a+0:0 sq+0:0 m1+1:0 a+0:1 sq+0:1 m1+1:1 a+0:2 sq+0:2 m1+1:2 a+0:3 sq+0:3 m1+1:3 nm+0 tz-1:0 tz-1:1 tz-1:2 d-1:0 tz-1:3 d-1:123 ta+3:01 ca+3:01 q1+2 r-2 e-3 gl-3 q2-2 m2-2 xb+2"
 
 
 def tile_transformerblock_pb_t_kernel(tc, attn, x, w_out, b_out, ln2_g, ln2_b, w1, b1, out_0, out_1):
@@ -75,10 +89,12 @@ def tile_transformerblock_pb_t_kernel(tc, attn, x, w_out, b_out, ln2_g, ln2_b, w
         w_raw = const.tile([P, 4, D], BF16)
         for u in range(n_units):
             n = SIZES[u]
+            if u == 0 and WFIRST:
+                nc.sync.dma_start(out=w_raw[:], in_=w_out.rearrange("(p t) d -> p t d", t=4))
             a_t = inp.tile([P, n, D], BF16, name="attn%d" % u)
             nc.sync.dma_start(out=a_t[:], in_=attn_v[:, first[u]:first[u] + n, :])
             T["attn", u] = a_t
-            if u == 0:
+            if u == 0 and not WFIRST:
                 nc.sync.dma_start(out=w_raw[:], in_=w_out.rearrange("(p t) d -> p t d", t=4))
             x_t = inp.tile([P, n, D], BF16, name="x%d" % u)
             nc.sync.dma_start(out=x_t[:], in_=x_v[:, first[u]:first[u] + n, :])
@@ -86,7 +102,7 @@ def tile_transformerblock_pb_t_kernel(tc, attn, x, w_out, b_out, ln2_g, ln2_b, w
             if u == CONST_AT:
                 for t in range(4):
                     nc.sync.dma_start(out=w1_raw[:, t, :], in_=w1.rearrange("(g t i) f -> t g i f", t=4, i=8)[t])
-                nc.sync.dma_start(out=crow[0:1, D:D + F], in_=b1.unsqueeze(0))
+                nc.sync.dma_start(out=(grow[8:9, :] if E2 else crow[0:1, D:D + F]), in_=b1.unsqueeze(0))
                 nc.sync.dma_start(out=grow[0:4, :], in_=ln2_g.rearrange("(g t i) -> t g i", t=4, i=8))
                 nc.sync.dma_start(out=grow[4:8, :], in_=ln2_b.rearrange("(g t i) -> t g i", t=4, i=8))
 
@@ -97,29 +113,42 @@ def tile_transformerblock_pb_t_kernel(tc, attn, x, w_out, b_out, ln2_g, ln2_b, w
         w1_codes = const.tile([P, F], U32, align_bytes=64)
         w1_scl = const.tile([P, F], U8, align_bytes=64)
         b1_sb = const.tile([P, 4, F], F32)
-        gb = const.tile([P, 8], F32)
+        gb = const.tile([P, 9], F32)
 
         if BPS:
             bo = psum.tile([P, D], F32, tag="bo", bufs=1)
-            nc.tensor.matmul(out=bo[:], lhsT=ones[:], rhs=crow[:, 0:D], start=True, stop=True)
         else:
-            bo_ps = psum.tile([P, D], F32, tag="mm1", bufs=MM1)
-            nc.tensor.matmul(out=bo_ps[:], lhsT=ones[:], rhs=crow[:, 0:D], start=True, stop=True)
             bo = const.tile([P, D], F32, name="bo")
-            nc.scalar.copy(out=bo[:], in_=bo_ps[:])
-        nc.vector.tensor_copy(out=w_grp[:].rearrange("q (c i) t -> q c t i", i=4),
-                              in_=w_raw[:].rearrange("q t (c i) -> q c t i", i=4))
+
+        def const_bo():
+            if BPS:
+                nc.tensor.matmul(out=bo[:], lhsT=ones[:], rhs=crow[:, 0:D], start=True, stop=True)
+                if GX:
+                    nc.scalar.copy(out=bo_sb[:], in_=bo[:])
+            else:
+                bo_ps = psum.tile([P, D], F32, tag="mm1", bufs=MM1)
+                nc.tensor.matmul(out=bo_ps[:], lhsT=ones[:], rhs=crow[:, 0:D], start=True, stop=True)
+                nc.scalar.copy(out=bo[:], in_=bo_ps[:])
+
+        bo_sb = const.tile([P, D], F32)
+        nc.vector.tensor_copy(out=w_grp[:, 0:D - WS].rearrange("q (c i) t -> q c t i", i=4),
+                              in_=w_raw[:, :, 0:D - WS].rearrange("q t (c i) -> q c t i", i=4))
+        if WS:
+            nc.scalar.copy(out=w_grp[:, D - WS:D].rearrange("q (c i) t -> q c t i", i=4),
+                           in_=w_raw[:, :, D - WS:D].rearrange("q t (c i) -> q c t i", i=4))
         nc.vector.quantize_mx(out=w_codes[:].bitcast(FP8X4), scales=w_scl[:],
                               in_=w_grp[:].rearrange("q d t -> q (d t)"))
 
         def consts_stage2():
-            b1_ps = psum.tile([P, D], F32, tag="mm1", bufs=MM1)
-            nc.tensor.matmul(out=b1_ps[:], lhsT=ones[:], rhs=crow[:, D:2 * D], start=True, stop=True)
+            if not E2:
+                b1_ps = psum.tile([P, D], F32, tag="mm1", bufs=MM1)
+                nc.tensor.matmul(out=b1_ps[:], lhsT=ones[:], rhs=crow[:, D:2 * D], start=True, stop=True)
             gb_ps = psum.tile([P, P], BF16, tag=MM2, bufs=TP if MM2 == "tp" else 1)
             nc.tensor.transpose(gb_ps[:], grow[:], ident_b[:])
-            nc.scalar.copy(out=b1_sb[:], in_=b1_ps[:, 0:F].unsqueeze(1).to_broadcast([P, 4, F]))
-            nc.scalar.copy(out=gb[:], in_=gb_ps[:, 0:8])
-            nc.vector.tensor_copy(out=w1_grp[:], in_=w1_raw[:].rearrange("q t f -> q f t"))
+            if not E2:
+                nc.scalar.copy(out=b1_sb[:], in_=b1_ps[:, 0:F].unsqueeze(1).to_broadcast([P, 4, F]))
+            nc.scalar.copy(out=gb[:], in_=gb_ps[:, 0:9])
+            (nc.vector.tensor_copy if W1V else nc.scalar.copy)(out=w1_grp[:], in_=w1_raw[:].rearrange("q t f -> q f t"))
             nc.vector.quantize_mx(out=w1_codes[:].bitcast(FP8X4), scales=w1_scl[:],
                                   in_=w1_grp[:].rearrange("q f t -> q (f t)"))
 
@@ -140,7 +169,7 @@ def tile_transformerblock_pb_t_kernel(tc, attn, x, w_out, b_out, ln2_g, ln2_b, w
             n = SIZES[u]
             m = min(2, n - 2 * h)
             if h == 0:
-                T["grp1", u] = work.tile([P, n * P * 4], BF16, align_bytes=64, tag="grp1", bufs=3, name="grp1")
+                T["grp1", u] = work.tile([P, n * P * 4], BF16, align_bytes=64, tag="grp1", bufs=AB, name="grp1")
             if m <= 0:
                 return
             g1f = T["grp1", u][:].bitcast(F32).rearrange("q (j r u) -> q j r u", j=n, u=2)
@@ -149,23 +178,24 @@ def tile_transformerblock_pb_t_kernel(tc, attn, x, w_out, b_out, ln2_g, ln2_b, w
 
         def st_q1(u):
             n = SIZES[u]
-            a_codes = work.tile([P, n * P], U32, align_bytes=64, tag="a_codes", bufs=3)
-            a_scl = work.tile([P, n * P], U8, align_bytes=64, tag="a_scl", bufs=3)
+            a_codes = work.tile([P, n * P], U32, align_bytes=64, tag="a_codes", bufs=AB)
+            a_scl = work.tile([P, n * P], U8, align_bytes=64, tag="a_scl", bufs=AB)
             nc.vector.quantize_mx(out=a_codes[:].bitcast(FP8X4), scales=a_scl[:], in_=T["grp1", u][:])
             T["a_codes", u] = a_codes
             T["a_scl", u] = a_scl
 
-        def st_xb(u, j):
+        def st_xb(u):
             n = SIZES[u]
-            if j == 0:
-                T["xm", u] = work.tile([P, n, D], F32, tag="xm", bufs=5, name="xm")
-            if j >= n:
-                return
-            xm = T["xm", u]
-            if XENG[j] == "G":
-                nc.gpsimd.tensor_tensor(out=xm[:, j, :], in0=T["x", u][:, j, :], in1=bo[:], op=ALU.add)
-            else:
-                nc.vector.tensor_tensor(out=xm[:, j, :], in0=bo[:], in1=T["x", u][:, j, :], op=ALU.add)
+            xm = work.tile([P, n, D], F32, tag="xm", bufs=XMB, name="xm")
+            T["xm", u] = xm
+            g = GX if n == 4 and u > 2 else 0
+            nc.vector.tensor_tensor(out=xm[:, g:n, :], in0=bo[:].unsqueeze(1).to_broadcast([P, n - g, D]), in1=T["x", u][:, g:n, :], op=ALU.add)
+
+        def st_gx(u):
+            n = SIZES[u]
+            g = GX if n == 4 and u > 2 else 0
+            for j in range(g):
+                nc.gpsimd.tensor_tensor(out=T["xm", u][:, j, :], in0=T["x", u][:, j, :], in1=bo_sb[:], op=ALU.add)
 
         def st_m1(u, j):
             if j >= SIZES[u]:
@@ -181,36 +211,39 @@ def tile_transformerblock_pb_t_kernel(tc, attn, x, w_out, b_out, ln2_g, ln2_b, w
             if j >= SIZES[u]:
                 return
             if j == 0:
-                T["sums", u] = work.tile([P, 4], F32, tag="sums", bufs=4, name="sums")
+                T["sums", u] = work.tile([P, 4], F32, tag="sums", bufs=NB, name="sums")
             xm = T["xm", u]
             nc.vector.scalar_tensor_tensor(out=xm[:, j, :], in0=T["mm1", u, j][:], scalar=0.0, in1=xm[:, j, :],
                                            op0=ALU.add, op1=ALU.add, accum_out=T["sums", u][:, j:j + 1])
 
         def st_nm(u):
             n = SIZES[u]
-            negmean = work.tile([P, 4], F32, tag="negmean", bufs=4)
-            if NMENG == "V":
-                nc.vector.tensor_scalar_mul(out=negmean[:, 0:n], in0=T["sums", u][:, 0:n], scalar1=-1.0 / D)
-            else:
-                nc.gpsimd.tensor_scalar(out=negmean[:, 0:n], in0=T["sums", u][:, 0:n], scalar1=-1.0 / D, scalar2=0.0, op0=ALU.mult, op1=ALU.add)
-            T["negmean", u] = negmean
             nc.sync.dma_start(out=xmid_v[:, first[u]:first[u] + n, :], in_=T["xm", u][:])
+            if not SUMB:
+                negmean = work.tile([P, 4], F32, tag="negmean", bufs=NB)
+                nc.vector.tensor_scalar_mul(out=negmean[:, 0:n], in0=T["sums", u][:, 0:n], scalar1=-1.0 / D)
+                T["negmean", u] = negmean
 
         def st_sq(u, j):
             if j == 0:
-                T["ssq", u] = work.tile([P, 4], F32, tag="ssq", bufs=4, name="ssq")
+                T["ssq", u] = work.tile([P, 4], F32, tag="ssq", bufs=NB, name="ssq")
             if j >= SIZES[u]:
                 return
             junk = work.tile([P, D], BF16, tag="junk", bufs=2)
-            nc.scalar.activation(out=junk[:], in_=T["xm", u][:, j, :], func=ACT.Square, bias=T["negmean", u][:, j:j + 1],
-                                 scale=1.0, accum_out=T["ssq", u][:, j:j + 1])
+            nc.scalar.activation(out=junk[:], in_=T["xm", u][:, j, :], func=ACT.Square, bias=T["sums" if SUMB else "negmean", u][:, j:j + 1],
+                                 scale=-1.0 * D if SUMB else 1.0, accum_out=T["ssq", u][:, j:j + 1])
 
         def st_pow(u):
             n = SIZES[u]
-            var = work.tile([P, 4], F32, tag="var", bufs=4)
-            nc.gpsimd.tensor_scalar(out=var[:, 0:n], in0=T["ssq", u][:, 0:n], scalar1=1.0 / D, scalar2=EPS,
+            var = work.tile([P, 4], F32, tag="var", bufs=NB)
+            if SUMB:
+                negmean = work.tile([P, 4], F32, tag="negmean", bufs=NB)
+                nc.gpsimd.tensor_scalar(out=negmean[:, 0:n], in0=T["sums", u][:, 0:n], scalar1=-1.0 / D, scalar2=0.0,
+                                        op0=ALU.mult, op1=ALU.add)
+                T["negmean", u] = negmean
+            nc.gpsimd.tensor_scalar(out=var[:, 0:n], in0=T["ssq", u][:, 0:n], scalar1=1.0 / (D * D * D) if SUMB else 1.0 / D, scalar2=EPS,
                                     op0=ALU.mult, op1=ALU.add)
-            rstd = work.tile([P, 4], F32, tag="rstd", bufs=4)
+            rstd = work.tile([P, 4], F32, tag="rstd", bufs=NB)
             nc.gpsimd.tensor_tensor(out=rstd[:, 0:n], in0=var[:, 0:n], in1=neghalf[:, 0:n], op=ALU.pow)
             T["rstd", u] = rstd
             if "S" in ZENG:
@@ -221,7 +254,7 @@ def tile_transformerblock_pb_t_kernel(tc, attn, x, w_out, b_out, ln2_g, ln2_b, w
         def st_z(u, j):
             n = SIZES[u]
             if j == 0:
-                T["z", u] = work.tile([P, n, D], F32, tag="z", bufs=2, name="z")
+                T["z", u] = work.tile([P, n, D], F32, tag="z", bufs=ZB, name="z")
             if j >= n:
                 return
             z = T["z", u]
@@ -241,7 +274,7 @@ def tile_transformerblock_pb_t_kernel(tc, attn, x, w_out, b_out, ln2_g, ln2_b, w
             if t0 % per_bank:
                 return
             if t0 == 0:
-                T["planes", u] = work.tile([P, 4, n * P], BF16, tag="planes", bufs=2, name="planes")
+                T["planes", u] = work.tile([P, 4, n * P], BF16, tag="planes", bufs=PB, name="planes")
             zt = psum.tile([P, D], F32, tag="tp", bufs=TP)
             for t in range(t0, t0 + per_bank):
                 for j in range(n):
@@ -262,15 +295,24 @@ def tile_transformerblock_pb_t_kernel(tc, attn, x, w_out, b_out, ln2_g, ln2_b, w
 
         def st_r(u):
             n = SIZES[u]
-            grp2 = work.tile([P, n * P, 4], BF16, align_bytes=64, tag="grp2", bufs=2)
-            T["grp2", u] = grp2
-            nc.vector.tensor_copy(out=grp2[:].rearrange("p (c i) t -> p c t i", i=4),
-                                  in_=T["planes", u][:].rearrange("p t (c i) -> p c t i", i=4))
+            if ("grp2", u) not in T:
+                T["grp2", u] = work.tile([P, n * P, 4], BF16, align_bytes=64, tag="grp2", bufs=PB, name="grp2")
+            grp2 = T["grp2", u]
+            k = n * P - (RS if n == 4 else 0)
+            nc.vector.tensor_copy(out=grp2[:, 0:k, :].rearrange("p (c i) t -> p c t i", i=4),
+                                  in_=T["planes", u][:, :, 0:k].rearrange("p t (c i) -> p c t i", i=4))
+
+        def st_rs(u):
+            n = SIZES[u]
+            if n == 4 and RS:
+                T["grp2", u] = work.tile([P, n * P, 4], BF16, align_bytes=64, tag="grp2", bufs=PB, name="grp2")
+                nc.scalar.copy(out=T["grp2", u][:, n * P - RS:n * P, :].rearrange("p (c i) t -> p c t i", i=4),
+                               in_=T["planes", u][:, :, n * P - RS:n * P].rearrange("p t (c i) -> p c t i", i=4))
 
         def st_q2(u):
             n = SIZES[u]
-            h_codes = work.tile([P, n * P], U32, align_bytes=64, tag="h_codes", bufs=2)
-            h_scl = work.tile([P, n * P], U8, align_bytes=64, tag="h_scl", bufs=2)
+            h_codes = work.tile([P, n * P], U32, align_bytes=64, tag="h_codes", bufs=PB)
+            h_scl = work.tile([P, n * P], U8, align_bytes=64, tag="h_scl", bufs=PB)
             nc.vector.quantize_mx(out=h_codes[:].bitcast(FP8X4), scales=h_scl[:],
                                   in_=T["grp2", u][:].rearrange("p r t -> p (r t)"))
             T["h_codes", u] = h_codes
@@ -280,31 +322,63 @@ def tile_transformerblock_pb_t_kernel(tc, attn, x, w_out, b_out, ln2_g, ln2_b, w
             n = SIZES[u]
             mm2 = psum.tile([P, n, F], F32, name="mm2", tag=MM2, bufs=TP if MM2 == "tp" else 1)
             T["mm2", u] = mm2
+            if E2:
+                nc.tensor.matmul_mx(out=mm2[:].rearrange("p n f -> p (n f)"), lhsT=w1_codes[:].bitcast(FP8X4), lhsT_scale=w1_scl[:],
+                                    rhs=T["h_codes", u][:].bitcast(FP8X4), rhs_scale=T["h_scl", u][:], start=True, stop=True)
+                return
             for j in range(n):
                 nc.tensor.matmul_mx(out=mm2[:, j, :], lhsT=T["h_codes", u][:, j * P:(j + 1) * P].bitcast(FP8X4),
                                     lhsT_scale=T["h_scl", u][:, j * P:(j + 1) * P],
                                     rhs=w1_codes[:].bitcast(FP8X4), rhs_scale=w1_scl[:], start=True, stop=True)
 
-        def st_e(u):
+        def st_th(u):
+            if not E2:
+                return
             n = SIZES[u]
-            pre = work.tile([P, n, F], F32, tag="pre", bufs=2)
+            ht = psum.tile([P, n, F], F32, tag="tp", bufs=TP)
+            T["ht", u] = ht
+            for j in range(n):
+                nc.tensor.transpose(ht[:, j, :], T["hidT", u][:, j, :], ident_f[:])
+
+        def st_ev(u):
+            if not E2:
+                return
+            n = SIZES[u]
+            hid = work.tile([P, n, F], F32, tag="hid", bufs=3)
+            if EVENG == "S":
+                nc.scalar.copy(out=hid[:], in_=T["ht", u][:])
+            else:
+                nc.vector.tensor_copy(out=hid[:], in_=T["ht", u][:])
+            nc.sync.dma_start(out=hid_v[:, first[u]:first[u] + n, :], in_=hid[:])
+
+        def st_e(u):
+            if E2:
+                return
+            n = SIZES[u]
+            pre = work.tile([P, n, F], F32, tag="pre", bufs=PB)
             nc.vector.tensor_tensor(out=pre[:], in0=T["mm2", u][:], in1=b1_sb[:, 0:n, :], op=ALU.add)
             T["pre", u] = pre
 
         def st_gl(u):
             n = SIZES[u]
+            if E2:
+                T["hidT", u] = work.tile([P, n, F], F32, tag="hidT", bufs=2, name="hidT")
+                nc.scalar.activation(out=T["hidT", u][:], in_=T["mm2", u][:], func=ACT.Gelu, bias=gb[:, 8:9])
+                return
             hid = work.tile([P, n, F], F32, tag="hid", bufs=3)
             nc.scalar.activation(out=hid[:], in_=T["pre", u][:], func=ACT.Gelu)
             nc.sync.dma_start(out=hid_v[:, first[u]:first[u] + n, :], in_=hid[:])
 
         fns = {"pow": st_pow, "z": st_z, "xb": st_xb, "nm": st_nm, "e": st_e, "sq": st_sq, "tz": st_tz, "d": st_d,
-               "ta": st_ta, "r": st_r, "q1": st_q1, "q2": st_q2, "m2": st_m2, "ca": st_ca, "gl": st_gl, "a": st_a, "m1": st_m1}
+               "ta": st_ta, "r": st_r, "gx": st_gx, "th": st_th, "ev": st_ev, "rs": st_rs, "q1": st_q1, "q2": st_q2, "m2": st_m2, "ca": st_ca, "gl": st_gl, "a": st_a, "m1": st_m1}
         steps = []
         for tok in ORDER.split(" "):
             body = tok.split(":")
             k = body[0].replace("+", " ").replace("-", " -").split(" ")
             steps.append((fns[k[0]], int(k[1]), [int(c) for c in body[1]] if len(body) > 1 else None))
-        for s in range(S0, n_units + 4):
+        for s in range(S0, n_units + TAIL):
+            if s == BO:
+                const_bo()
             if s == C2:
                 consts_stage2()
             for f, o, js in steps:

@@ -20,14 +20,14 @@ FLOPS = 2 * TOK * D * D + 2 * TOK * D * F
 SIZES = (2, 2, 4, 4, 4, 4, 4, 4, 2, 2)
 CA_AHEAD = 3
 XB_AHEAD = 2
-ZENG = "GGGG"
+ZENG = "GSGS"
 XMB = 5
 BPS = True
 MM1 = 4
 TP = 3
 DUP = 0
 MM2 = "tp"
-ZLAST = 3
+ZLAST = 2
 NMENG = "V"
 CONST_AT = 2
 C2 = 0
@@ -36,17 +36,26 @@ BO = -2
 WS = 0
 WFIRST = False
 RS = 0
+MERGE = 0
+CROW_Y = False
+GXU = ()
+RSU = ()
+DV = 0
+DLAST = 2
+W1_AT = 2
+C3 = 0
 SUMB = True
 GX = 0
+GXMIN = 0
 NB = 4
 ZB = 2
 PB = 2
 AB = 3
 TAIL = 4
 E2 = False
-EVENG = "S"
+EVL = 0
 W1V = True
-ORDER = "pow-1 z-1:0123 a+0:0 sq+0:0 m1+1:0 a+0:1 sq+0:1 m1+1:1 a+0:2 sq+0:2 m1+1:2 a+0:3 sq+0:3 m1+1:3 nm+0 tz-1:0 tz-1:1 tz-1:2 d-1:0 tz-1:3 d-1:123 ta+3:01 ca+3:01 q1+2 r-2 e-3 gl-3 q2-2 m2-2 xb+2"
+ORDER = "pow-1 z-1:0123 a+0:0 sq+0:0 m1+1:0 a+0:1 sq+0:1 m1+1:1 a+0:2 sq+0:2 m1+1:2 a+0:3 sq+0:3 m1+1:3 zv-1:0123 nm+0 zs-1:0123 ta+3:01 ca+3:01 tz-1:0 tz-1:1 tz-1:2 d-1:0 tz-1:3 d-1:123 r-2 e-3 gl-3 q1+2 q2-2 m2-2 xb+2"
 
 
 def tile_transformerblock_pb_t_kernel(tc, attn, x, w_out, b_out, ln2_g, ln2_b, w1, b1, out_0, out_1):
@@ -72,8 +81,10 @@ def tile_transformerblock_pb_t_kernel(tc, attn, x, w_out, b_out, ln2_g, ln2_b, w
         make_identity(nc, ident_f[:])
         ident_b = const.tile([P, P], BF16)
         make_identity(nc, ident_b[:])
-        crow = const.tile([P, 2 * D], BF16)
+        crow = const.tile([P, D], BF16)
         nc.vector.memset(crow[:], 0.0)
+        b1row = const.tile([P, F], BF16)
+        nc.vector.memset(b1row[:], 0.0)
         grow = const.tile([P, P], BF16)
         nc.vector.memset(grow[:], 0.0)
         ones = const.tile([P, P], BF16)
@@ -82,10 +93,23 @@ def tile_transformerblock_pb_t_kernel(tc, attn, x, w_out, b_out, ln2_g, ln2_b, w
         nc.vector.memset(neghalf[:], -0.5)
         warm = const.tile([P, 2], F32)
         nc.vector.memset(warm[:], 0.0)
-        nc.scalar.dma_start(out=crow[0:1, 0:D], in_=b_out.unsqueeze(0))
+        if not CROW_Y:
+            nc.scalar.dma_start(out=crow[0:1, 0:D], in_=b_out.unsqueeze(0))
         w1_raw = const.tile([P, 4, F], BF16)
         nc.scalar.activation(out=warm[:, 1:2], in_=warm[:, 0:1], func=ACT.Gelu)
 
+        def w1_loads(q):
+            for t in range(4):
+                q.dma_start(out=w1_raw[:, t, :], in_=w1.rearrange("(g t i) f -> t g i f", t=4, i=8)[t])
+
+        def small_loads(q):
+            q.dma_start(out=(grow[8:9, :] if E2 else b1row[0:1, :]), in_=b1.unsqueeze(0))
+            q.dma_start(out=grow[0:4, :], in_=ln2_g.rearrange("(g t i) -> t g i", t=4, i=8))
+            q.dma_start(out=grow[4:8, :], in_=ln2_b.rearrange("(g t i) -> t g i", t=4, i=8))
+
+        if CONST_AT < 0:
+            small_loads(nc.gpsimd)
+            w1_loads(nc.gpsimd)
         w_raw = const.tile([P, 4, D], BF16)
         for u in range(n_units):
             n = SIZES[u]
@@ -96,15 +120,15 @@ def tile_transformerblock_pb_t_kernel(tc, attn, x, w_out, b_out, ln2_g, ln2_b, w
             T["attn", u] = a_t
             if u == 0 and not WFIRST:
                 nc.sync.dma_start(out=w_raw[:], in_=w_out.rearrange("(p t) d -> p t d", t=4))
+            if u == 0 and CROW_Y:
+                nc.sync.dma_start(out=crow[0:1, 0:D], in_=b_out.unsqueeze(0))
             x_t = inp.tile([P, n, D], BF16, name="x%d" % u)
             nc.sync.dma_start(out=x_t[:], in_=x_v[:, first[u]:first[u] + n, :])
             T["x", u] = x_t
             if u == CONST_AT:
-                for t in range(4):
-                    nc.sync.dma_start(out=w1_raw[:, t, :], in_=w1.rearrange("(g t i) f -> t g i f", t=4, i=8)[t])
-                nc.sync.dma_start(out=(grow[8:9, :] if E2 else crow[0:1, D:D + F]), in_=b1.unsqueeze(0))
-                nc.sync.dma_start(out=grow[0:4, :], in_=ln2_g.rearrange("(g t i) -> t g i", t=4, i=8))
-                nc.sync.dma_start(out=grow[4:8, :], in_=ln2_b.rearrange("(g t i) -> t g i", t=4, i=8))
+                small_loads(nc.sync)
+            if u == W1_AT:
+                w1_loads(nc.sync)
 
         w_grp = const.tile([P, D, 4], BF16, align_bytes=64)
         w_codes = const.tile([P, D], U32, align_bytes=64)
@@ -123,7 +147,7 @@ def tile_transformerblock_pb_t_kernel(tc, attn, x, w_out, b_out, ln2_g, ln2_b, w
         def const_bo():
             if BPS:
                 nc.tensor.matmul(out=bo[:], lhsT=ones[:], rhs=crow[:, 0:D], start=True, stop=True)
-                if GX:
+                if GX or GXU:
                     nc.scalar.copy(out=bo_sb[:], in_=bo[:])
             else:
                 bo_ps = psum.tile([P, D], F32, tag="mm1", bufs=MM1)
@@ -142,12 +166,14 @@ def tile_transformerblock_pb_t_kernel(tc, attn, x, w_out, b_out, ln2_g, ln2_b, w
         def consts_stage2():
             if not E2:
                 b1_ps = psum.tile([P, D], F32, tag="mm1", bufs=MM1)
-                nc.tensor.matmul(out=b1_ps[:], lhsT=ones[:], rhs=crow[:, D:2 * D], start=True, stop=True)
+                nc.tensor.matmul(out=b1_ps[:, 0:F], lhsT=ones[:], rhs=b1row[:], start=True, stop=True)
             gb_ps = psum.tile([P, P], BF16, tag=MM2, bufs=TP if MM2 == "tp" else 1)
             nc.tensor.transpose(gb_ps[:], grow[:], ident_b[:])
             if not E2:
                 nc.scalar.copy(out=b1_sb[:], in_=b1_ps[:, 0:F].unsqueeze(1).to_broadcast([P, 4, F]))
             nc.scalar.copy(out=gb[:], in_=gb_ps[:, 0:9])
+
+        def const_w1():
             (nc.vector.tensor_copy if W1V else nc.scalar.copy)(out=w1_grp[:], in_=w1_raw[:].rearrange("q t f -> q f t"))
             nc.vector.quantize_mx(out=w1_codes[:].bitcast(FP8X4), scales=w1_scl[:],
                                   in_=w1_grp[:].rearrange("q f t -> q (f t)"))
@@ -188,12 +214,16 @@ def tile_transformerblock_pb_t_kernel(tc, attn, x, w_out, b_out, ln2_g, ln2_b, w
             n = SIZES[u]
             xm = work.tile([P, n, D], F32, tag="xm", bufs=XMB, name="xm")
             T["xm", u] = xm
-            g = GX if n == 4 and u > 2 else 0
+            if u in GXU:
+                for j in range(n):
+                    nc.gpsimd.tensor_tensor(out=xm[:, j, :], in0=T["x", u][:, j, :], in1=bo_sb[:], op=ALU.add)
+                return
+            g = GX if n == 4 and u >= GXMIN else 0
             nc.vector.tensor_tensor(out=xm[:, g:n, :], in0=bo[:].unsqueeze(1).to_broadcast([P, n - g, D]), in1=T["x", u][:, g:n, :], op=ALU.add)
 
         def st_gx(u):
             n = SIZES[u]
-            g = GX if n == 4 and u > 2 else 0
+            g = GX if n == 4 and u >= GXMIN else 0
             for j in range(g):
                 nc.gpsimd.tensor_tensor(out=T["xm", u][:, j, :], in0=T["x", u][:, j, :], in1=bo_sb[:], op=ALU.add)
 
@@ -255,10 +285,20 @@ def tile_transformerblock_pb_t_kernel(tc, attn, x, w_out, b_out, ln2_g, ln2_b, w
             n = SIZES[u]
             if j == 0:
                 T["z", u] = work.tile([P, n, D], F32, tag="z", bufs=ZB, name="z")
-            if j >= n:
+            if j >= n or u >= len(SIZES) - ZLAST or ZENG[j] != "G":
                 return
+            z_tile(u, j, ZENG[j])
+
+        def st_zs(u, j):
+            if j < SIZES[u] and u < len(SIZES) - ZLAST and ZENG[j] == "S":
+                z_tile(u, j, "S")
+
+        def st_zv(u, j):
+            if j < SIZES[u] and (u >= len(SIZES) - ZLAST or ZENG[j] == "V"):
+                z_tile(u, j, "V")
+
+        def z_tile(u, j, k):
             z = T["z", u]
-            k = "V" if u >= len(SIZES) - ZLAST else ZENG[j]
             o = z[:, j, :].rearrange("p (t g i) -> p t g i", t=4, i=8)
             xv = T["xm", u][:, j, :].rearrange("p (g t i) -> p t g i", t=4, i=8)
             if k == "S":
@@ -290,8 +330,20 @@ def tile_transformerblock_pb_t_kernel(tc, attn, x, w_out, b_out, ln2_g, ln2_b, w
             zt = T["zt", u, t0]
             for t in range(t0, t0 + per_bank):
                 c0 = (t - t0) * n * P
+                if u >= len(SIZES) - DLAST and t >= 4 - DV:
+                    continue
                 nc.scalar.activation(out=T["planes", u][:, t, :], in_=zt[:, c0:c0 + n * P], func=ACT.Identity,
                                      bias=gb[:, 4 + t:5 + t], scale=gb[:, t:t + 1])
+
+        def st_dv(u):
+            n = SIZES[u]
+            per_bank = 4 // n
+            for t in range(4 - DV, 4):
+                if u >= len(SIZES) - DLAST:
+                    zt = T["zt", u, t // per_bank * per_bank]
+                    c0 = (t % per_bank) * n * P
+                    nc.vector.tensor_scalar(out=T["planes", u][:, t, :], in0=zt[:, c0:c0 + n * P], scalar1=gb[:, t:t + 1],
+                                            scalar2=gb[:, 4 + t:5 + t], op0=ALU.mult, op1=ALU.add)
 
         def st_r(u):
             n = SIZES[u]
@@ -299,12 +351,18 @@ def tile_transformerblock_pb_t_kernel(tc, attn, x, w_out, b_out, ln2_g, ln2_b, w
                 T["grp2", u] = work.tile([P, n * P, 4], BF16, align_bytes=64, tag="grp2", bufs=PB, name="grp2")
             grp2 = T["grp2", u]
             k = n * P - (RS if n == 4 else 0)
+            if u in RSU:
+                return
             nc.vector.tensor_copy(out=grp2[:, 0:k, :].rearrange("p (c i) t -> p c t i", i=4),
                                   in_=T["planes", u][:, :, 0:k].rearrange("p t (c i) -> p c t i", i=4))
 
         def st_rs(u):
             n = SIZES[u]
-            if n == 4 and RS:
+            if u in RSU:
+                T["grp2", u] = work.tile([P, n * P, 4], BF16, align_bytes=64, tag="grp2", bufs=PB, name="grp2")
+                nc.scalar.copy(out=T["grp2", u][:].rearrange("p (c i) t -> p c t i", i=4),
+                               in_=T["planes", u][:].rearrange("p t (c i) -> p c t i", i=4))
+            elif n == 4 and RS:
                 T["grp2", u] = work.tile([P, n * P, 4], BF16, align_bytes=64, tag="grp2", bufs=PB, name="grp2")
                 nc.scalar.copy(out=T["grp2", u][:, n * P - RS:n * P, :].rearrange("p (c i) t -> p c t i", i=4),
                                in_=T["planes", u][:, :, n * P - RS:n * P].rearrange("p t (c i) -> p c t i", i=4))
@@ -345,7 +403,7 @@ def tile_transformerblock_pb_t_kernel(tc, attn, x, w_out, b_out, ln2_g, ln2_b, w
                 return
             n = SIZES[u]
             hid = work.tile([P, n, F], F32, tag="hid", bufs=3)
-            if EVENG == "S":
+            if u < len(SIZES) - EVL:
                 nc.scalar.copy(out=hid[:], in_=T["ht", u][:])
             else:
                 nc.vector.tensor_copy(out=hid[:], in_=T["ht", u][:])
@@ -370,20 +428,27 @@ def tile_transformerblock_pb_t_kernel(tc, attn, x, w_out, b_out, ln2_g, ln2_b, w
             nc.sync.dma_start(out=hid_v[:, first[u]:first[u] + n, :], in_=hid[:])
 
         fns = {"pow": st_pow, "z": st_z, "xb": st_xb, "nm": st_nm, "e": st_e, "sq": st_sq, "tz": st_tz, "d": st_d,
-               "ta": st_ta, "r": st_r, "gx": st_gx, "th": st_th, "ev": st_ev, "rs": st_rs, "q1": st_q1, "q2": st_q2, "m2": st_m2, "ca": st_ca, "gl": st_gl, "a": st_a, "m1": st_m1}
+               "ta": st_ta, "r": st_r, "dv": st_dv, "zv": st_zv, "zs": st_zs, "gx": st_gx, "th": st_th, "ev": st_ev, "rs": st_rs, "q1": st_q1, "q2": st_q2, "m2": st_m2, "ca": st_ca, "gl": st_gl, "a": st_a, "m1": st_m1}
         steps = []
         for tok in ORDER.split(" "):
             body = tok.split(":")
             k = body[0].replace("+", " ").replace("-", " -").split(" ")
             steps.append((fns[k[0]], int(k[1]), [int(c) for c in body[1]] if len(body) > 1 else None))
+        step_of = list(range(n_units))
+        for u in range(n_units - MERGE, n_units):
+            step_of[u] -= 1
         for s in range(S0, n_units + TAIL):
             if s == BO:
                 const_bo()
             if s == C2:
                 consts_stage2()
+            if s == C3:
+                const_w1()
             for f, o, js in steps:
-                if ok(s + o):
-                    if js is None:
-                        f(s + o)
-                    for j in js or []:
-                        f(s + o, j)
+                us = [u for u in range(n_units) if step_of[u] == s + o]
+                if js is None:
+                    for u in us:
+                        f(u)
+                for j in js or []:
+                    for u in us:
+                        f(u, j)

@@ -17,10 +17,10 @@ F = 128
 NT = TOK // P
 EPS = 1e-5
 FLOPS = 2 * TOK * D * D + 2 * TOK * D * F
-SIZES = (2, 2, 4, 4, 4, 4, 4, 4, 2, 2)
+SIZES = (2, 4, 4, 4, 4, 4, 4, 4, 2)
 CA_AHEAD = 3
 XB_AHEAD = 2
-ZENG = "GSGS"
+ZENG = "GGGS"
 XMB = 5
 BPS = True
 MM1 = 4
@@ -38,7 +38,7 @@ WFIRST = False
 RS = 0
 MERGE = 0
 CROW_Y = False
-GXU = ()
+GXU = (1,)
 RSU = ()
 DV = 0
 DLAST = 2
@@ -55,7 +55,7 @@ TAIL = 4
 E2 = False
 EVL = 0
 W1V = True
-ORDER = "pow-1 z-1:0123 a+0:0 sq+0:0 m1+1:0 a+0:1 sq+0:1 m1+1:1 a+0:2 sq+0:2 m1+1:2 a+0:3 sq+0:3 m1+1:3 zv-1:0123 nm+0 zs-1:0123 ta+3:01 ca+3:01 tz-1:0 tz-1:1 tz-1:2 d-1:0 tz-1:3 d-1:123 r-2 e-3 gl-3 q1+2 q2-2 m2-2 xb+2"
+ORDER = "pow-1 z-1:0123 zs-1:0123 a+0:0 sq+0:0 m1+1:0 a+0:1 sq+0:1 m1+1:1 a+0:2 sq+0:2 m1+1:2 a+0:3 sq+0:3 m1+1:3 zv-1:0123 nm+0 tz-1:0 tz-1:1 tz-1:2 d-1:0 tz-1:3 d-1:123 ta+3:01 ca+3:01 r-2 e-3 gl-3 q1+2 q2-2 m2-2 xb+2"
 
 
 def tile_transformerblock_pb_t_kernel(tc, attn, x, w_out, b_out, ln2_g, ln2_b, w1, b1, out_0, out_1):

@@ -10,6 +10,7 @@ U8 = mybir.dt.uint8
 FP8X4 = mybir.dt.float8_e4m3fn_x4
 ALU = mybir.AluOpType
 ACT = mybir.ActivationFunctionType
+
 P = 128
 TOK = 4096
 D = 512
@@ -17,45 +18,11 @@ F = 128
 NT = TOK // P
 EPS = 1e-5
 FLOPS = 2 * TOK * D * D + 2 * TOK * D * F
-SIZES = (2, 4, 4, 4, 4, 4, 4, 4, 2)
-CA_AHEAD = 3
-XB_AHEAD = 2
-ZENG = "GGGS"
-XMB = 5
-BPS = True
-MM1 = 4
-TP = 3
-DUP = 0
-MM2 = "tp"
-ZLAST = 2
-NMENG = "V"
-CONST_AT = 2
-C2 = 0
-S0 = -4
-BO = -2
-WS = 0
-WFIRST = False
-RS = 0
-MERGE = 0
-CROW_Y = False
-GXU = (1,)
-RSU = ()
-DV = 0
-DLAST = 2
-W1_AT = 2
-C3 = 0
-SUMB = True
-GX = 0
-GXMIN = 0
-NB = 4
-ZB = 2
-PB = 2
-AB = 3
-TAIL = 4
-E2 = False
-EVL = 0
-W1V = True
-ORDER = "pow-1 z-1:0123 zs-1:0123 a+0:0 sq+0:0 m1+1:0 a+0:1 sq+0:1 m1+1:1 a+0:2 sq+0:2 m1+1:2 a+0:3 sq+0:3 m1+1:3 zv-1:0123 nm+0 tz-1:0 tz-1:1 tz-1:2 d-1:0 tz-1:3 d-1:123 ta+3:01 ca+3:01 r-2 e-3 gl-3 q1+2 q2-2 m2-2 xb+2"
+
+UNITS = (2, 4, 4, 4, 4, 4, 4, 4, 2)
+GPSIMD_BIAS_UNIT = 1
+SCALAR_Z_TILE = 3
+VECTOR_Z_UNITS = 2
 
 
 def tile_transformerblock_pb_t_kernel(tc, attn, x, w_out, b_out, ln2_g, ln2_b, w1, b1, out_0, out_1):
@@ -64,71 +31,58 @@ def tile_transformerblock_pb_t_kernel(tc, attn, x, w_out, b_out, ln2_g, ln2_b, w
     x_v = x.flatten_outer_dims().rearrange("(p n) k -> p n k", n=NT)
     xmid_v = out_0.flatten_outer_dims().rearrange("(p n) k -> p n k", n=NT)
     hid_v = out_1.flatten_outer_dims().rearrange("(p n) k -> p n k", n=NT)
-    n_units = len(SIZES)
-    first = [sum(SIZES[:u]) for u in range(n_units)]
+    n_units = len(UNITS)
+    first = [sum(UNITS[:u]) for u in range(n_units)]
+
     with ExitStack() as ctx:
         const = ctx.enter_context(tc.tile_pool(name="const", bufs=1))
         inp = ctx.enter_context(tc.tile_pool(name="inp", bufs=1))
         work = ctx.enter_context(tc.tile_pool(name="work", bufs=2))
-        psum = ctx.enter_context(tc.psum_pool(name="psum", bufs=2))
+        psum = ctx.enter_context(tc.psum_pool(name="psum", bufs=1))
         ctx.enter_context(tc.manual_schedule())
+
         T = {}
 
-        def ok(u):
-            return 0 <= u < n_units
+        def bank(name):
+            return psum.tile([P, D], F32, tag=name, bufs={"mm1": 4, "tp": 3, "bo": 1}[name], name=name)
 
         ident_f = const.tile([P, P], F32)
         make_identity(nc, ident_f[:])
         ident_b = const.tile([P, P], BF16)
         make_identity(nc, ident_b[:])
-        crow = const.tile([P, D], BF16)
-        nc.vector.memset(crow[:], 0.0)
-        b1row = const.tile([P, F], BF16)
-        nc.vector.memset(b1row[:], 0.0)
-        grow = const.tile([P, P], BF16)
-        nc.vector.memset(grow[:], 0.0)
+
+        bo_row = const.tile([P, D], BF16)
+        nc.vector.memset(bo_row[:], 0.0)
+        b1_row = const.tile([P, F], BF16)
+        nc.vector.memset(b1_row[:], 0.0)
+        gb_rows = const.tile([P, P], BF16)
+        nc.vector.memset(gb_rows[:], 0.0)
         ones = const.tile([P, P], BF16)
         nc.vector.memset(ones[:], 1.0)
         neghalf = const.tile([P, 4], F32)
         nc.vector.memset(neghalf[:], -0.5)
         warm = const.tile([P, 2], F32)
         nc.vector.memset(warm[:], 0.0)
-        if not CROW_Y:
-            nc.scalar.dma_start(out=crow[0:1, 0:D], in_=b_out.unsqueeze(0))
-        w1_raw = const.tile([P, 4, F], BF16)
+        nc.scalar.dma_start(out=bo_row[0:1, :], in_=b_out.unsqueeze(0))
         nc.scalar.activation(out=warm[:, 1:2], in_=warm[:, 0:1], func=ACT.Gelu)
 
-        def w1_loads(q):
-            for t in range(4):
-                q.dma_start(out=w1_raw[:, t, :], in_=w1.rearrange("(g t i) f -> t g i f", t=4, i=8)[t])
-
-        def small_loads(q):
-            q.dma_start(out=(grow[8:9, :] if E2 else b1row[0:1, :]), in_=b1.unsqueeze(0))
-            q.dma_start(out=grow[0:4, :], in_=ln2_g.rearrange("(g t i) -> t g i", t=4, i=8))
-            q.dma_start(out=grow[4:8, :], in_=ln2_b.rearrange("(g t i) -> t g i", t=4, i=8))
-
-        if CONST_AT < 0:
-            small_loads(nc.gpsimd)
-            w1_loads(nc.gpsimd)
         w_raw = const.tile([P, 4, D], BF16)
+        w1_raw = const.tile([P, 4, F], BF16)
         for u in range(n_units):
-            n = SIZES[u]
-            if u == 0 and WFIRST:
+            n = UNITS[u]
+            T["attn", u] = inp.tile([P, n, D], BF16, name="attn%d" % u)
+            nc.sync.dma_start(out=T["attn", u][:], in_=attn_v[:, first[u]:first[u] + n, :])
+            if u == 0:
                 nc.sync.dma_start(out=w_raw[:], in_=w_out.rearrange("(p t) d -> p t d", t=4))
-            a_t = inp.tile([P, n, D], BF16, name="attn%d" % u)
-            nc.sync.dma_start(out=a_t[:], in_=attn_v[:, first[u]:first[u] + n, :])
-            T["attn", u] = a_t
-            if u == 0 and not WFIRST:
-                nc.sync.dma_start(out=w_raw[:], in_=w_out.rearrange("(p t) d -> p t d", t=4))
-            if u == 0 and CROW_Y:
-                nc.sync.dma_start(out=crow[0:1, 0:D], in_=b_out.unsqueeze(0))
-            x_t = inp.tile([P, n, D], BF16, name="x%d" % u)
-            nc.sync.dma_start(out=x_t[:], in_=x_v[:, first[u]:first[u] + n, :])
-            T["x", u] = x_t
-            if u == CONST_AT:
-                small_loads(nc.sync)
-            if u == W1_AT:
-                w1_loads(nc.sync)
+            T["x", u] = inp.tile([P, n, D], BF16, name="x%d" % u)
+            nc.sync.dma_start(out=T["x", u][:], in_=x_v[:, first[u]:first[u] + n, :])
+            if u == 2:
+                nc.sync.dma_start(out=b1_row[0:1, :], in_=b1.unsqueeze(0))
+                nc.sync.dma_start(out=gb_rows[0:4, :], in_=ln2_g.rearrange("(g t i) -> t g i", t=4, i=8))
+                nc.sync.dma_start(out=gb_rows[4:8, :], in_=ln2_b.rearrange("(g t i) -> t g i", t=4, i=8))
+                w1_v = w1.rearrange("(g t i) f -> t g i f", t=4, i=8)
+                for t in range(4):
+                    nc.sync.dma_start(out=w1_raw[:, t, :], in_=w1_v[t])
 
         w_grp = const.tile([P, D, 4], BF16, align_bytes=64)
         w_codes = const.tile([P, D], U32, align_bytes=64)
@@ -137,318 +91,217 @@ def tile_transformerblock_pb_t_kernel(tc, attn, x, w_out, b_out, ln2_g, ln2_b, w
         w1_codes = const.tile([P, F], U32, align_bytes=64)
         w1_scl = const.tile([P, F], U8, align_bytes=64)
         b1_sb = const.tile([P, 4, F], F32)
-        gb = const.tile([P, 9], F32)
-
-        if BPS:
-            bo = psum.tile([P, D], F32, tag="bo", bufs=1)
-        else:
-            bo = const.tile([P, D], F32, name="bo")
-
-        def const_bo():
-            if BPS:
-                nc.tensor.matmul(out=bo[:], lhsT=ones[:], rhs=crow[:, 0:D], start=True, stop=True)
-                if GX or GXU:
-                    nc.scalar.copy(out=bo_sb[:], in_=bo[:])
-            else:
-                bo_ps = psum.tile([P, D], F32, tag="mm1", bufs=MM1)
-                nc.tensor.matmul(out=bo_ps[:], lhsT=ones[:], rhs=crow[:, 0:D], start=True, stop=True)
-                nc.scalar.copy(out=bo[:], in_=bo_ps[:])
-
+        gb = const.tile([P, 8], F32)
         bo_sb = const.tile([P, D], F32)
-        nc.vector.tensor_copy(out=w_grp[:, 0:D - WS].rearrange("q (c i) t -> q c t i", i=4),
-                              in_=w_raw[:, :, 0:D - WS].rearrange("q t (c i) -> q c t i", i=4))
-        if WS:
-            nc.scalar.copy(out=w_grp[:, D - WS:D].rearrange("q (c i) t -> q c t i", i=4),
-                           in_=w_raw[:, :, D - WS:D].rearrange("q t (c i) -> q c t i", i=4))
+        bo = bank("bo")
+
+        def regroup(out, in_):
+            nc.vector.tensor_copy(out=out.rearrange("q (c i) t -> q c t i", i=4),
+                                  in_=in_.rearrange("q t (c i) -> q c t i", i=4))
+
+        regroup(w_grp[:], w_raw[:])
         nc.vector.quantize_mx(out=w_codes[:].bitcast(FP8X4), scales=w_scl[:],
                               in_=w_grp[:].rearrange("q d t -> q (d t)"))
 
-        def consts_stage2():
-            if not E2:
-                b1_ps = psum.tile([P, D], F32, tag="mm1", bufs=MM1)
-                nc.tensor.matmul(out=b1_ps[:, 0:F], lhsT=ones[:], rhs=b1row[:], start=True, stop=True)
-            gb_ps = psum.tile([P, P], BF16, tag=MM2, bufs=TP if MM2 == "tp" else 1)
-            nc.tensor.transpose(gb_ps[:], grow[:], ident_b[:])
-            if not E2:
-                nc.scalar.copy(out=b1_sb[:], in_=b1_ps[:, 0:F].unsqueeze(1).to_broadcast([P, 4, F]))
-            nc.scalar.copy(out=gb[:], in_=gb_ps[:, 0:9])
+        def const_b_out():
+            nc.tensor.matmul(out=bo[:], lhsT=ones[:], rhs=bo_row[:], start=True, stop=True)
+            nc.scalar.copy(out=bo_sb[:], in_=bo[:])
 
-        def const_w1():
-            (nc.vector.tensor_copy if W1V else nc.scalar.copy)(out=w1_grp[:], in_=w1_raw[:].rearrange("q t f -> q f t"))
+        def const_stage_2():
+            b1_ps = bank("mm1")
+            nc.tensor.matmul(out=b1_ps[:, 0:F], lhsT=ones[:], rhs=b1_row[:], start=True, stop=True)
+            gb_ps = psum.tile([P, P], BF16, tag="tp", bufs=3)
+            nc.tensor.transpose(gb_ps[:], gb_rows[:], ident_b[:])
+            nc.scalar.copy(out=b1_sb[:], in_=b1_ps[:, 0:F].unsqueeze(1).to_broadcast([P, 4, F]))
+            nc.scalar.copy(out=gb[:], in_=gb_ps[:, 0:8])
+            nc.vector.tensor_copy(out=w1_grp[:], in_=w1_raw[:].rearrange("q t f -> q f t"))
             nc.vector.quantize_mx(out=w1_codes[:].bitcast(FP8X4), scales=w1_scl[:],
                                   in_=w1_grp[:].rearrange("q f t -> q (f t)"))
 
-        def st_ta(u, h):
-            n = SIZES[u]
-            m = min(2, n - 2 * h)
-            if m <= 0:
-                return
-            tpa = psum.tile([P, D], F32, tag="tp", bufs=TP)
-            for jj in range(m):
-                words = T["attn", u][:, 2 * h + jj, :].bitcast(F32)
-                for uu in range(2):
-                    c0 = (2 * jj + uu) * P
-                    nc.tensor.transpose(tpa[:, c0:c0 + P], words[:, uu:2 * P:2], ident_f[:])
-            T["tpa", u, h] = tpa
+        def transpose_attn(u, pair):
+            ps = bank("tp")
+            for j in range(2):
+                words = T["attn", u][:, 2 * pair + j, :].bitcast(F32)
+                for s in range(2):
+                    c0 = (2 * j + s) * P
+                    nc.tensor.transpose(ps[:, c0:c0 + P], words[:, s:2 * P:2], ident_f[:])
+            T["attn_t", u, pair] = ps
 
-        def st_ca(u, h):
-            n = SIZES[u]
-            m = min(2, n - 2 * h)
-            if h == 0:
-                T["grp1", u] = work.tile([P, n * P * 4], BF16, align_bytes=64, tag="grp1", bufs=AB, name="grp1")
-            if m <= 0:
-                return
-            g1f = T["grp1", u][:].bitcast(F32).rearrange("q (j r u) -> q j r u", j=n, u=2)
-            nc.scalar.copy(out=g1f[:, 2 * h:2 * h + m, :, :],
-                           in_=T["tpa", u, h][:, 0:m * 2 * P].rearrange("q (j u r) -> q j r u", j=m, u=2))
+        def copy_attn(u, pair):
+            n = UNITS[u]
+            if pair == 0:
+                T["a_grp", u] = work.tile([P, n * P * 4], BF16, align_bytes=64, tag="a_grp", bufs=3, name="a_grp")
+            words = T["a_grp", u][:].bitcast(F32).rearrange("q (j r s) -> q j r s", j=n, s=2)
+            nc.scalar.copy(out=words[:, 2 * pair:2 * pair + 2, :, :],
+                           in_=T["attn_t", u, pair][:].rearrange("q (j s r) -> q j r s", j=2, s=2))
 
-        def st_q1(u):
-            n = SIZES[u]
-            a_codes = work.tile([P, n * P], U32, align_bytes=64, tag="a_codes", bufs=AB)
-            a_scl = work.tile([P, n * P], U8, align_bytes=64, tag="a_scl", bufs=AB)
-            nc.vector.quantize_mx(out=a_codes[:].bitcast(FP8X4), scales=a_scl[:], in_=T["grp1", u][:])
-            T["a_codes", u] = a_codes
-            T["a_scl", u] = a_scl
+        def quantise_attn(u):
+            n = UNITS[u]
+            T["a_codes", u] = work.tile([P, n * P], U32, align_bytes=64, tag="a_codes", bufs=3, name="a_codes")
+            T["a_scl", u] = work.tile([P, n * P], U8, align_bytes=64, tag="a_scl", bufs=3, name="a_scl")
+            nc.vector.quantize_mx(out=T["a_codes", u][:].bitcast(FP8X4), scales=T["a_scl", u][:], in_=T["a_grp", u][:])
 
-        def st_xb(u):
-            n = SIZES[u]
-            xm = work.tile([P, n, D], F32, tag="xm", bufs=XMB, name="xm")
-            T["xm", u] = xm
-            if u in GXU:
+        def add_b_out(u):
+            n = UNITS[u]
+            T["xm", u] = work.tile([P, n, D], F32, tag="xm", bufs=5, name="xm")
+            if u == GPSIMD_BIAS_UNIT:
                 for j in range(n):
-                    nc.gpsimd.tensor_tensor(out=xm[:, j, :], in0=T["x", u][:, j, :], in1=bo_sb[:], op=ALU.add)
-                return
-            g = GX if n == 4 and u >= GXMIN else 0
-            nc.vector.tensor_tensor(out=xm[:, g:n, :], in0=bo[:].unsqueeze(1).to_broadcast([P, n - g, D]), in1=T["x", u][:, g:n, :], op=ALU.add)
-
-        def st_gx(u):
-            n = SIZES[u]
-            g = GX if n == 4 and u >= GXMIN else 0
-            for j in range(g):
-                nc.gpsimd.tensor_tensor(out=T["xm", u][:, j, :], in0=T["x", u][:, j, :], in1=bo_sb[:], op=ALU.add)
-
-        def st_m1(u, j):
-            if j >= SIZES[u]:
-                return
-            mm1 = psum.tile([P, D], F32, tag="mm1", bufs=MM1)
-            for rep in range(1 + (DUP if isinstance(DUP, int) else DUP[j % len(DUP)])):
-                nc.tensor.matmul_mx(out=mm1[:], lhsT=T["a_codes", u][:, j * P:(j + 1) * P].bitcast(FP8X4),
-                                lhsT_scale=T["a_scl", u][:, j * P:(j + 1) * P],
-                                rhs=w_codes[:].bitcast(FP8X4), rhs_scale=w_scl[:], start=True, stop=True)
-            T["mm1", u, j] = mm1
-
-        def st_a(u, j):
-            if j >= SIZES[u]:
-                return
-            if j == 0:
-                T["sums", u] = work.tile([P, 4], F32, tag="sums", bufs=NB, name="sums")
-            xm = T["xm", u]
-            nc.vector.scalar_tensor_tensor(out=xm[:, j, :], in0=T["mm1", u, j][:], scalar=0.0, in1=xm[:, j, :],
-                                           op0=ALU.add, op1=ALU.add, accum_out=T["sums", u][:, j:j + 1])
-
-        def st_nm(u):
-            n = SIZES[u]
-            nc.sync.dma_start(out=xmid_v[:, first[u]:first[u] + n, :], in_=T["xm", u][:])
-            if not SUMB:
-                negmean = work.tile([P, 4], F32, tag="negmean", bufs=NB)
-                nc.vector.tensor_scalar_mul(out=negmean[:, 0:n], in0=T["sums", u][:, 0:n], scalar1=-1.0 / D)
-                T["negmean", u] = negmean
-
-        def st_sq(u, j):
-            if j == 0:
-                T["ssq", u] = work.tile([P, 4], F32, tag="ssq", bufs=NB, name="ssq")
-            if j >= SIZES[u]:
-                return
-            junk = work.tile([P, D], BF16, tag="junk", bufs=2)
-            nc.scalar.activation(out=junk[:], in_=T["xm", u][:, j, :], func=ACT.Square, bias=T["sums" if SUMB else "negmean", u][:, j:j + 1],
-                                 scale=-1.0 * D if SUMB else 1.0, accum_out=T["ssq", u][:, j:j + 1])
-
-        def st_pow(u):
-            n = SIZES[u]
-            var = work.tile([P, 4], F32, tag="var", bufs=NB)
-            if SUMB:
-                negmean = work.tile([P, 4], F32, tag="negmean", bufs=NB)
-                nc.gpsimd.tensor_scalar(out=negmean[:, 0:n], in0=T["sums", u][:, 0:n], scalar1=-1.0 / D, scalar2=0.0,
-                                        op0=ALU.mult, op1=ALU.add)
-                T["negmean", u] = negmean
-            nc.gpsimd.tensor_scalar(out=var[:, 0:n], in0=T["ssq", u][:, 0:n], scalar1=1.0 / (D * D * D) if SUMB else 1.0 / D, scalar2=EPS,
-                                    op0=ALU.mult, op1=ALU.add)
-            rstd = work.tile([P, 4], F32, tag="rstd", bufs=NB)
-            nc.gpsimd.tensor_tensor(out=rstd[:, 0:n], in0=var[:, 0:n], in1=neghalf[:, 0:n], op=ALU.pow)
-            T["rstd", u] = rstd
-            if "S" in ZENG:
-                nmr = work.tile([P, 4], F32, tag="nmr", bufs=4)
-                nc.gpsimd.tensor_tensor(out=nmr[:, 0:n], in0=T["negmean", u][:, 0:n], in1=rstd[:, 0:n], op=ALU.mult)
-                T["nmr", u] = nmr
-
-        def st_z(u, j):
-            n = SIZES[u]
-            if j == 0:
-                T["z", u] = work.tile([P, n, D], F32, tag="z", bufs=ZB, name="z")
-            if j >= n or u >= len(SIZES) - ZLAST or ZENG[j] != "G":
-                return
-            z_tile(u, j, ZENG[j])
-
-        def st_zs(u, j):
-            if j < SIZES[u] and u < len(SIZES) - ZLAST and ZENG[j] == "S":
-                z_tile(u, j, "S")
-
-        def st_zv(u, j):
-            if j < SIZES[u] and (u >= len(SIZES) - ZLAST or ZENG[j] == "V"):
-                z_tile(u, j, "V")
-
-        def z_tile(u, j, k):
-            z = T["z", u]
-            o = z[:, j, :].rearrange("p (t g i) -> p t g i", t=4, i=8)
-            xv = T["xm", u][:, j, :].rearrange("p (g t i) -> p t g i", t=4, i=8)
-            if k == "S":
-                nc.scalar.activation(out=o, in_=xv, func=ACT.Identity, bias=T["nmr", u][:, j:j + 1], scale=T["rstd", u][:, j:j + 1])
+                    nc.gpsimd.tensor_tensor(out=T["xm", u][:, j, :], in0=T["x", u][:, j, :], in1=bo_sb[:], op=ALU.add)
             else:
-                eng = nc.gpsimd if k == "G" else nc.vector
-                eng.tensor_scalar(out=o, in0=xv, scalar1=T["negmean", u][:, j:j + 1],
-                                  scalar2=T["rstd", u][:, j:j + 1], op0=ALU.add, op1=ALU.mult)
+                nc.vector.tensor_tensor(out=T["xm", u][:], in0=bo[:].unsqueeze(1).to_broadcast([P, n, D]),
+                                        in1=T["x", u][:], op=ALU.add)
 
-        def st_tz(u, t0):
-            n = SIZES[u]
-            per_bank = 4 // n
-            if t0 % per_bank:
-                return
+        def product_1(u, j):
+            T["mm1", u, j] = bank("mm1")
+            cols = slice(j * P, (j + 1) * P)
+            nc.tensor.matmul_mx(out=T["mm1", u, j][:], lhsT=T["a_codes", u][:, cols].bitcast(FP8X4),
+                                lhsT_scale=T["a_scl", u][:, cols], rhs=w_codes[:].bitcast(FP8X4), rhs_scale=w_scl[:],
+                                start=True, stop=True)
+
+        def residual(u, j):
+            if j == 0:
+                T["sums", u] = work.tile([P, 4], F32, tag="sums", bufs=4, name="sums")
+            xm = T["xm", u][:, j, :]
+            nc.vector.scalar_tensor_tensor(out=xm, in0=T["mm1", u, j][:], scalar=0.0, in1=xm, op0=ALU.add, op1=ALU.add,
+                                           accum_out=T["sums", u][:, j:j + 1])
+
+        def squares(u, j):
+            if j == 0:
+                T["ssq", u] = work.tile([P, 4], F32, tag="ssq", bufs=4, name="ssq")
+            unread = work.tile([P, D], BF16, tag="unread", bufs=2)
+            nc.scalar.activation(out=unread[:], in_=T["xm", u][:, j, :], func=ACT.Square,
+                                 bias=T["sums", u][:, j:j + 1], scale=-1.0 * D, accum_out=T["ssq", u][:, j:j + 1])
+
+        def store_x_mid(u):
+            nc.sync.dma_start(out=xmid_v[:, first[u]:first[u] + UNITS[u], :], in_=T["xm", u][:])
+
+        def z_engine(u, j):
+            if u >= n_units - VECTOR_Z_UNITS:
+                return "vector"
+            return "scalar" if j == SCALAR_Z_TILE else "gpsimd"
+
+        def statistics(u):
+            n = UNITS[u]
+            T["negmean", u] = work.tile([P, 4], F32, tag="negmean", bufs=4, name="negmean")
+            nc.gpsimd.tensor_scalar(out=T["negmean", u][:, 0:n], in0=T["sums", u][:, 0:n], scalar1=-1.0 / D,
+                                    scalar2=0.0, op0=ALU.mult, op1=ALU.add)
+            var = work.tile([P, 4], F32, tag="var", bufs=4)
+            nc.gpsimd.tensor_scalar(out=var[:, 0:n], in0=T["ssq", u][:, 0:n], scalar1=1.0 / (D * D * D), scalar2=EPS,
+                                    op0=ALU.mult, op1=ALU.add)
+            T["rstd", u] = work.tile([P, 4], F32, tag="rstd", bufs=4, name="rstd")
+            nc.gpsimd.tensor_tensor(out=T["rstd", u][:, 0:n], in0=var[:, 0:n], in1=neghalf[:, 0:n], op=ALU.pow)
+            for j in range(n):
+                if z_engine(u, j) == "scalar":
+                    T["shift", u] = work.tile([P, 1], F32, tag="shift", bufs=4, name="shift")
+                    nc.gpsimd.tensor_tensor(out=T["shift", u][:], in0=T["negmean", u][:, j:j + 1],
+                                            in1=T["rstd", u][:, j:j + 1], op=ALU.mult)
+
+        def normalise(u, engine):
+            n = UNITS[u]
+            if engine == "gpsimd":
+                T["z", u] = work.tile([P, n, D], F32, tag="z", bufs=2, name="z")
+            for j in range(n):
+                if z_engine(u, j) != engine:
+                    continue
+                out = T["z", u][:, j, :].rearrange("p (t g i) -> p t g i", t=4, i=8)
+                in_ = T["xm", u][:, j, :].rearrange("p (g t i) -> p t g i", t=4, i=8)
+                rstd = T["rstd", u][:, j:j + 1]
+                if engine == "scalar":
+                    nc.scalar.activation(out=out, in_=in_, func=ACT.Identity, bias=T["shift", u][:], scale=rstd)
+                else:
+                    eng = nc.gpsimd if engine == "gpsimd" else nc.vector
+                    eng.tensor_scalar(out=out, in0=in_, scalar1=T["negmean", u][:, j:j + 1], scalar2=rstd,
+                                      op0=ALU.add, op1=ALU.mult)
+
+        def transpose_z(u, t0):
+            n = UNITS[u]
             if t0 == 0:
-                T["planes", u] = work.tile([P, 4, n * P], BF16, tag="planes", bufs=PB, name="planes")
-            zt = psum.tile([P, D], F32, tag="tp", bufs=TP)
-            for t in range(t0, t0 + per_bank):
+                T["planes", u] = work.tile([P, 4, n * P], BF16, tag="planes", bufs=2, name="planes")
+            T["z_t", u, t0] = bank("tp")
+            for t in range(t0, t0 + 4 // n):
                 for j in range(n):
                     c0 = ((t - t0) * n + j) * P
-                    nc.tensor.transpose(zt[:, c0:c0 + P], T["z", u][:, j, t * P:(t + 1) * P], ident_f[:])
-            T["zt", u, t0] = zt
+                    nc.tensor.transpose(T["z_t", u, t0][:, c0:c0 + P], T["z", u][:, j, t * P:(t + 1) * P], ident_f[:])
 
-        def st_d(u, t0):
-            n = SIZES[u]
-            per_bank = 4 // n
-            if t0 % per_bank:
-                return
-            zt = T["zt", u, t0]
-            for t in range(t0, t0 + per_bank):
+        def gain_bias(u, t0):
+            n = UNITS[u]
+            for t in range(t0, t0 + 4 // n):
                 c0 = (t - t0) * n * P
-                if u >= len(SIZES) - DLAST and t >= 4 - DV:
-                    continue
-                nc.scalar.activation(out=T["planes", u][:, t, :], in_=zt[:, c0:c0 + n * P], func=ACT.Identity,
-                                     bias=gb[:, 4 + t:5 + t], scale=gb[:, t:t + 1])
+                nc.scalar.activation(out=T["planes", u][:, t, :], in_=T["z_t", u, t0][:, c0:c0 + n * P],
+                                     func=ACT.Identity, bias=gb[:, 4 + t:5 + t], scale=gb[:, t:t + 1])
 
-        def st_dv(u):
-            n = SIZES[u]
-            per_bank = 4 // n
-            for t in range(4 - DV, 4):
-                if u >= len(SIZES) - DLAST:
-                    zt = T["zt", u, t // per_bank * per_bank]
-                    c0 = (t % per_bank) * n * P
-                    nc.vector.tensor_scalar(out=T["planes", u][:, t, :], in0=zt[:, c0:c0 + n * P], scalar1=gb[:, t:t + 1],
-                                            scalar2=gb[:, 4 + t:5 + t], op0=ALU.mult, op1=ALU.add)
+        def regroup_h2(u):
+            T["h_grp", u] = work.tile([P, UNITS[u] * P, 4], BF16, align_bytes=64, tag="h_grp", bufs=2, name="h_grp")
+            regroup(T["h_grp", u][:], T["planes", u][:])
 
-        def st_r(u):
-            n = SIZES[u]
-            if ("grp2", u) not in T:
-                T["grp2", u] = work.tile([P, n * P, 4], BF16, align_bytes=64, tag="grp2", bufs=PB, name="grp2")
-            grp2 = T["grp2", u]
-            k = n * P - (RS if n == 4 else 0)
-            if u in RSU:
-                return
-            nc.vector.tensor_copy(out=grp2[:, 0:k, :].rearrange("p (c i) t -> p c t i", i=4),
-                                  in_=T["planes", u][:, :, 0:k].rearrange("p t (c i) -> p c t i", i=4))
+        def quantise_h2(u):
+            n = UNITS[u]
+            T["h_codes", u] = work.tile([P, n * P], U32, align_bytes=64, tag="h_codes", bufs=2, name="h_codes")
+            T["h_scl", u] = work.tile([P, n * P], U8, align_bytes=64, tag="h_scl", bufs=2, name="h_scl")
+            nc.vector.quantize_mx(out=T["h_codes", u][:].bitcast(FP8X4), scales=T["h_scl", u][:],
+                                  in_=T["h_grp", u][:].rearrange("p r t -> p (r t)"))
 
-        def st_rs(u):
-            n = SIZES[u]
-            if u in RSU:
-                T["grp2", u] = work.tile([P, n * P, 4], BF16, align_bytes=64, tag="grp2", bufs=PB, name="grp2")
-                nc.scalar.copy(out=T["grp2", u][:].rearrange("p (c i) t -> p c t i", i=4),
-                               in_=T["planes", u][:].rearrange("p t (c i) -> p c t i", i=4))
-            elif n == 4 and RS:
-                T["grp2", u] = work.tile([P, n * P, 4], BF16, align_bytes=64, tag="grp2", bufs=PB, name="grp2")
-                nc.scalar.copy(out=T["grp2", u][:, n * P - RS:n * P, :].rearrange("p (c i) t -> p c t i", i=4),
-                               in_=T["planes", u][:, :, n * P - RS:n * P].rearrange("p t (c i) -> p c t i", i=4))
-
-        def st_q2(u):
-            n = SIZES[u]
-            h_codes = work.tile([P, n * P], U32, align_bytes=64, tag="h_codes", bufs=PB)
-            h_scl = work.tile([P, n * P], U8, align_bytes=64, tag="h_scl", bufs=PB)
-            nc.vector.quantize_mx(out=h_codes[:].bitcast(FP8X4), scales=h_scl[:],
-                                  in_=T["grp2", u][:].rearrange("p r t -> p (r t)"))
-            T["h_codes", u] = h_codes
-            T["h_scl", u] = h_scl
-
-        def st_m2(u):
-            n = SIZES[u]
-            mm2 = psum.tile([P, n, F], F32, name="mm2", tag=MM2, bufs=TP if MM2 == "tp" else 1)
-            T["mm2", u] = mm2
-            if E2:
-                nc.tensor.matmul_mx(out=mm2[:].rearrange("p n f -> p (n f)"), lhsT=w1_codes[:].bitcast(FP8X4), lhsT_scale=w1_scl[:],
-                                    rhs=T["h_codes", u][:].bitcast(FP8X4), rhs_scale=T["h_scl", u][:], start=True, stop=True)
-                return
+        def product_2(u):
+            n = UNITS[u]
+            T["mm2", u] = psum.tile([P, n, F], F32, tag="tp", bufs=3, name="mm2")
             for j in range(n):
-                nc.tensor.matmul_mx(out=mm2[:, j, :], lhsT=T["h_codes", u][:, j * P:(j + 1) * P].bitcast(FP8X4),
-                                    lhsT_scale=T["h_scl", u][:, j * P:(j + 1) * P],
-                                    rhs=w1_codes[:].bitcast(FP8X4), rhs_scale=w1_scl[:], start=True, stop=True)
+                cols = slice(j * P, (j + 1) * P)
+                nc.tensor.matmul_mx(out=T["mm2", u][:, j, :], lhsT=T["h_codes", u][:, cols].bitcast(FP8X4),
+                                    lhsT_scale=T["h_scl", u][:, cols], rhs=w1_codes[:].bitcast(FP8X4),
+                                    rhs_scale=w1_scl[:], start=True, stop=True)
 
-        def st_th(u):
-            if not E2:
-                return
-            n = SIZES[u]
-            ht = psum.tile([P, n, F], F32, tag="tp", bufs=TP)
-            T["ht", u] = ht
-            for j in range(n):
-                nc.tensor.transpose(ht[:, j, :], T["hidT", u][:, j, :], ident_f[:])
+        def add_b1(u):
+            n = UNITS[u]
+            T["pre", u] = work.tile([P, n, F], F32, tag="pre", bufs=2, name="pre")
+            nc.vector.tensor_tensor(out=T["pre", u][:], in0=T["mm2", u][:], in1=b1_sb[:, 0:n, :], op=ALU.add)
 
-        def st_ev(u):
-            if not E2:
-                return
-            n = SIZES[u]
-            hid = work.tile([P, n, F], F32, tag="hid", bufs=3)
-            if u < len(SIZES) - EVL:
-                nc.scalar.copy(out=hid[:], in_=T["ht", u][:])
-            else:
-                nc.vector.tensor_copy(out=hid[:], in_=T["ht", u][:])
-            nc.sync.dma_start(out=hid_v[:, first[u]:first[u] + n, :], in_=hid[:])
-
-        def st_e(u):
-            if E2:
-                return
-            n = SIZES[u]
-            pre = work.tile([P, n, F], F32, tag="pre", bufs=PB)
-            nc.vector.tensor_tensor(out=pre[:], in0=T["mm2", u][:], in1=b1_sb[:, 0:n, :], op=ALU.add)
-            T["pre", u] = pre
-
-        def st_gl(u):
-            n = SIZES[u]
-            if E2:
-                T["hidT", u] = work.tile([P, n, F], F32, tag="hidT", bufs=2, name="hidT")
-                nc.scalar.activation(out=T["hidT", u][:], in_=T["mm2", u][:], func=ACT.Gelu, bias=gb[:, 8:9])
-                return
+        def gelu(u):
+            n = UNITS[u]
             hid = work.tile([P, n, F], F32, tag="hid", bufs=3)
             nc.scalar.activation(out=hid[:], in_=T["pre", u][:], func=ACT.Gelu)
             nc.sync.dma_start(out=hid_v[:, first[u]:first[u] + n, :], in_=hid[:])
 
-        fns = {"pow": st_pow, "z": st_z, "xb": st_xb, "nm": st_nm, "e": st_e, "sq": st_sq, "tz": st_tz, "d": st_d,
-               "ta": st_ta, "r": st_r, "dv": st_dv, "zv": st_zv, "zs": st_zs, "gx": st_gx, "th": st_th, "ev": st_ev, "rs": st_rs, "q1": st_q1, "q2": st_q2, "m2": st_m2, "ca": st_ca, "gl": st_gl, "a": st_a, "m1": st_m1}
-        steps = []
-        for tok in ORDER.split(" "):
-            body = tok.split(":")
-            k = body[0].replace("+", " ").replace("-", " -").split(" ")
-            steps.append((fns[k[0]], int(k[1]), [int(c) for c in body[1]] if len(body) > 1 else None))
-        step_of = list(range(n_units))
-        for u in range(n_units - MERGE, n_units):
-            step_of[u] -= 1
-        for s in range(S0, n_units + TAIL):
-            if s == BO:
-                const_bo()
-            if s == C2:
-                consts_stage2()
-            if s == C3:
-                const_w1()
-            for f, o, js in steps:
-                us = [u for u in range(n_units) if step_of[u] == s + o]
-                if js is None:
-                    for u in us:
-                        f(u)
-                for j in js or []:
-                    for u in us:
-                        f(u, j)
+        def each(u, f, *indices):
+            if 0 <= u < n_units:
+                for i in indices:
+                    f(u, i)
+
+        def whole(u, f):
+            if 0 <= u < n_units:
+                f(u)
+
+        def tiles(u):
+            return UNITS[u] if 0 <= u < n_units else 0
+
+        for s in range(-3, n_units + 4):
+            if s == -2:
+                const_b_out()
+            if s == 0:
+                const_stage_2()
+            whole(s - 1, statistics)
+            each(s - 1, normalise, "gpsimd", "scalar")
+            for j in range(4):
+                if j < tiles(s):
+                    residual(s, j)
+                    squares(s, j)
+                if j < tiles(s + 1) and s >= -1:
+                    product_1(s + 1, j)
+            each(s - 1, normalise, "vector")
+            whole(s - 4, add_b1)
+            whole(s, store_x_mid)
+            if tiles(s - 1):
+                values = range(0, 4, 4 // tiles(s - 1))
+                each(s - 1, transpose_z, *values[:3])
+                each(s - 1, gain_bias, values[0])
+                each(s - 1, transpose_z, *values[3:])
+                each(s - 1, gain_bias, *values[1:])
+            whole(s - 4, gelu)
+            for pair in range(tiles(s + 3) // 2):
+                transpose_attn(s + 3, pair)
+            whole(s - 3, product_2)
+            for pair in range(tiles(s + 3) // 2):
+                copy_attn(s + 3, pair)
+            whole(s - 2, regroup_h2)
+            whole(s + 2, quantise_attn)
+            whole(s - 2, quantise_h2)
+            whole(s + 2, add_b_out)

from contextlib import ExitStack

import concourse.mybir as mybir
from concourse.masks import make_identity

F32 = mybir.dt.float32
BF16 = mybir.dt.bfloat16
U32 = mybir.dt.uint32
U8 = mybir.dt.uint8
FP8X4 = mybir.dt.float8_e4m3fn_x4
ALU = mybir.AluOpType
ACT = mybir.ActivationFunctionType

P = 128
TOK = 4096
D = 512
F = 128
NT = TOK // P
EPS = 1e-5
FLOPS = 2 * TOK * D * D + 2 * TOK * D * F

UNITS = (2, 4, 4, 4, 4, 4, 4, 4, 2)
GPSIMD_BIAS_UNIT = 1
SCALAR_Z_TILE = 3
VECTOR_Z_UNITS = 2


def tile_transformerblock_pb_t_kernel(tc, attn, x, w_out, b_out, ln2_g, ln2_b, w1, b1, out_0, out_1):
    nc = tc.nc
    attn_v = attn.flatten_outer_dims().rearrange("(p n) k -> p n k", n=NT)
    x_v = x.flatten_outer_dims().rearrange("(p n) k -> p n k", n=NT)
    xmid_v = out_0.flatten_outer_dims().rearrange("(p n) k -> p n k", n=NT)
    hid_v = out_1.flatten_outer_dims().rearrange("(p n) k -> p n k", n=NT)
    n_units = len(UNITS)
    first = [sum(UNITS[:u]) for u in range(n_units)]

    with ExitStack() as ctx:
        const = ctx.enter_context(tc.tile_pool(name="const", bufs=1))
        inp = ctx.enter_context(tc.tile_pool(name="inp", bufs=1))
        work = ctx.enter_context(tc.tile_pool(name="work", bufs=2))
        psum = ctx.enter_context(tc.psum_pool(name="psum", bufs=1))
        ctx.enter_context(tc.manual_schedule())

        T = {}

        def bank(name):
            return psum.tile([P, D], F32, tag=name, bufs={"mm1": 4, "tp": 3, "bo": 1}[name], name=name)

        ident_f = const.tile([P, P], F32)
        make_identity(nc, ident_f[:])
        ident_b = const.tile([P, P], BF16)
        make_identity(nc, ident_b[:])

        bo_row = const.tile([P, D], BF16)
        nc.vector.memset(bo_row[:], 0.0)
        b1_row = const.tile([P, F], BF16)
        nc.vector.memset(b1_row[:], 0.0)
        gb_rows = const.tile([P, P], BF16)
        nc.vector.memset(gb_rows[:], 0.0)
        ones = const.tile([P, P], BF16)
        nc.vector.memset(ones[:], 1.0)
        neghalf = const.tile([P, 4], F32)
        nc.vector.memset(neghalf[:], -0.5)
        warm = const.tile([P, 2], F32)
        nc.vector.memset(warm[:], 0.0)
        nc.scalar.dma_start(out=bo_row[0:1, :], in_=b_out.unsqueeze(0))
        nc.scalar.activation(out=warm[:, 1:2], in_=warm[:, 0:1], func=ACT.Gelu)

        w_raw = const.tile([P, 4, D], BF16)
        w1_raw = const.tile([P, 4, F], BF16)
        for u in range(n_units):
            n = UNITS[u]
            T["attn", u] = inp.tile([P, n, D], BF16, name="attn%d" % u)
            nc.sync.dma_start(out=T["attn", u][:], in_=attn_v[:, first[u]:first[u] + n, :])
            if u == 0:
                nc.sync.dma_start(out=w_raw[:], in_=w_out.rearrange("(p t) d -> p t d", t=4))
            T["x", u] = inp.tile([P, n, D], BF16, name="x%d" % u)
            nc.sync.dma_start(out=T["x", u][:], in_=x_v[:, first[u]:first[u] + n, :])
            if u == 2:
                nc.sync.dma_start(out=b1_row[0:1, :], in_=b1.unsqueeze(0))
                nc.sync.dma_start(out=gb_rows[0:4, :], in_=ln2_g.rearrange("(g t i) -> t g i", t=4, i=8))
                nc.sync.dma_start(out=gb_rows[4:8, :], in_=ln2_b.rearrange("(g t i) -> t g i", t=4, i=8))
                w1_v = w1.rearrange("(g t i) f -> t g i f", t=4, i=8)
                for t in range(4):
                    nc.sync.dma_start(out=w1_raw[:, t, :], in_=w1_v[t])

        w_grp = const.tile([P, D, 4], BF16, align_bytes=64)
        w_codes = const.tile([P, D], U32, align_bytes=64)
        w_scl = const.tile([P, D], U8, align_bytes=64)
        w1_grp = const.tile([P, F, 4], BF16, align_bytes=64)
        w1_codes = const.tile([P, F], U32, align_bytes=64)
        w1_scl = const.tile([P, F], U8, align_bytes=64)
        b1_sb = const.tile([P, 4, F], F32)
        gb = const.tile([P, 8], F32)
        bo_sb = const.tile([P, D], F32)
        bo = bank("bo")

        def regroup(out, in_):
            nc.vector.tensor_copy(out=out.rearrange("q (c i) t -> q c t i", i=4),
                                  in_=in_.rearrange("q t (c i) -> q c t i", i=4))

        regroup(w_grp[:], w_raw[:])
        nc.vector.quantize_mx(out=w_codes[:].bitcast(FP8X4), scales=w_scl[:],
                              in_=w_grp[:].rearrange("q d t -> q (d t)"))

        def const_b_out():
            nc.tensor.matmul(out=bo[:], lhsT=ones[:], rhs=bo_row[:], start=True, stop=True)
            nc.scalar.copy(out=bo_sb[:], in_=bo[:])

        def const_stage_2():
            b1_ps = bank("mm1")
            nc.tensor.matmul(out=b1_ps[:, 0:F], lhsT=ones[:], rhs=b1_row[:], start=True, stop=True)
            gb_ps = psum.tile([P, P], BF16, tag="tp", bufs=3)
            nc.tensor.transpose(gb_ps[:], gb_rows[:], ident_b[:])
            nc.scalar.copy(out=b1_sb[:], in_=b1_ps[:, 0:F].unsqueeze(1).to_broadcast([P, 4, F]))
            nc.scalar.copy(out=gb[:], in_=gb_ps[:, 0:8])
            nc.vector.tensor_copy(out=w1_grp[:], in_=w1_raw[:].rearrange("q t f -> q f t"))
            nc.vector.quantize_mx(out=w1_codes[:].bitcast(FP8X4), scales=w1_scl[:],
                                  in_=w1_grp[:].rearrange("q f t -> q (f t)"))

        def transpose_attn(u, pair):
            ps = bank("tp")
            for j in range(2):
                words = T["attn", u][:, 2 * pair + j, :].bitcast(F32)
                for s in range(2):
                    c0 = (2 * j + s) * P
                    nc.tensor.transpose(ps[:, c0:c0 + P], words[:, s:2 * P:2], ident_f[:])
            T["attn_t", u, pair] = ps

        def copy_attn(u, pair):
            n = UNITS[u]
            if pair == 0:
                T["a_grp", u] = work.tile([P, n * P * 4], BF16, align_bytes=64, tag="a_grp", bufs=3, name="a_grp")
            words = T["a_grp", u][:].bitcast(F32).rearrange("q (j r s) -> q j r s", j=n, s=2)
            nc.scalar.copy(out=words[:, 2 * pair:2 * pair + 2, :, :],
                           in_=T["attn_t", u, pair][:].rearrange("q (j s r) -> q j r s", j=2, s=2))

        def quantise_attn(u):
            n = UNITS[u]
            T["a_codes", u] = work.tile([P, n * P], U32, align_bytes=64, tag="a_codes", bufs=3, name="a_codes")
            T["a_scl", u] = work.tile([P, n * P], U8, align_bytes=64, tag="a_scl", bufs=3, name="a_scl")
            nc.vector.quantize_mx(out=T["a_codes", u][:].bitcast(FP8X4), scales=T["a_scl", u][:], in_=T["a_grp", u][:])

        def add_b_out(u):
            n = UNITS[u]
            T["xm", u] = work.tile([P, n, D], F32, tag="xm", bufs=5, name="xm")
            if u == GPSIMD_BIAS_UNIT:
                for j in range(n):
                    nc.gpsimd.tensor_tensor(out=T["xm", u][:, j, :], in0=T["x", u][:, j, :], in1=bo_sb[:], op=ALU.add)
            else:
                nc.vector.tensor_tensor(out=T["xm", u][:], in0=bo[:].unsqueeze(1).to_broadcast([P, n, D]),
                                        in1=T["x", u][:], op=ALU.add)

        def product_1(u, j):
            T["mm1", u, j] = bank("mm1")
            cols = slice(j * P, (j + 1) * P)
            nc.tensor.matmul_mx(out=T["mm1", u, j][:], lhsT=T["a_codes", u][:, cols].bitcast(FP8X4),
                                lhsT_scale=T["a_scl", u][:, cols], rhs=w_codes[:].bitcast(FP8X4), rhs_scale=w_scl[:],
                                start=True, stop=True)

        def residual(u, j):
            if j == 0:
                T["sums", u] = work.tile([P, 4], F32, tag="sums", bufs=4, name="sums")
            xm = T["xm", u][:, j, :]
            nc.vector.scalar_tensor_tensor(out=xm, in0=T["mm1", u, j][:], scalar=0.0, in1=xm, op0=ALU.add, op1=ALU.add,
                                           accum_out=T["sums", u][:, j:j + 1])

        def squares(u, j):
            if j == 0:
                T["ssq", u] = work.tile([P, 4], F32, tag="ssq", bufs=4, name="ssq")
            unread = work.tile([P, D], BF16, tag="unread", bufs=2)
            nc.scalar.activation(out=unread[:], in_=T["xm", u][:, j, :], func=ACT.Square,
                                 bias=T["sums", u][:, j:j + 1], scale=-1.0 * D, accum_out=T["ssq", u][:, j:j + 1])

        def store_x_mid(u):
            nc.sync.dma_start(out=xmid_v[:, first[u]:first[u] + UNITS[u], :], in_=T["xm", u][:])

        def z_engine(u, j):
            if u >= n_units - VECTOR_Z_UNITS:
                return "vector"
            return "scalar" if j == SCALAR_Z_TILE else "gpsimd"

        def statistics(u):
            n = UNITS[u]
            T["negmean", u] = work.tile([P, 4], F32, tag="negmean", bufs=4, name="negmean")
            nc.gpsimd.tensor_scalar(out=T["negmean", u][:, 0:n], in0=T["sums", u][:, 0:n], scalar1=-1.0 / D,
                                    scalar2=0.0, op0=ALU.mult, op1=ALU.add)
            var = work.tile([P, 4], F32, tag="var", bufs=4)
            nc.gpsimd.tensor_scalar(out=var[:, 0:n], in0=T["ssq", u][:, 0:n], scalar1=1.0 / (D * D * D), scalar2=EPS,
                                    op0=ALU.mult, op1=ALU.add)
            T["rstd", u] = work.tile([P, 4], F32, tag="rstd", bufs=4, name="rstd")
            nc.gpsimd.tensor_tensor(out=T["rstd", u][:, 0:n], in0=var[:, 0:n], in1=neghalf[:, 0:n], op=ALU.pow)
            for j in range(n):
                if z_engine(u, j) == "scalar":
                    T["shift", u] = work.tile([P, 1], F32, tag="shift", bufs=4, name="shift")
                    nc.gpsimd.tensor_tensor(out=T["shift", u][:], in0=T["negmean", u][:, j:j + 1],
                                            in1=T["rstd", u][:, j:j + 1], op=ALU.mult)

        def normalise(u, engine):
            n = UNITS[u]
            if engine == "gpsimd":
                T["z", u] = work.tile([P, n, D], F32, tag="z", bufs=2, name="z")
            for j in range(n):
                if z_engine(u, j) != engine:
                    continue
                out = T["z", u][:, j, :].rearrange("p (t g i) -> p t g i", t=4, i=8)
                in_ = T["xm", u][:, j, :].rearrange("p (g t i) -> p t g i", t=4, i=8)
                rstd = T["rstd", u][:, j:j + 1]
                if engine == "scalar":
                    nc.scalar.activation(out=out, in_=in_, func=ACT.Identity, bias=T["shift", u][:], scale=rstd)
                else:
                    eng = nc.gpsimd if engine == "gpsimd" else nc.vector
                    eng.tensor_scalar(out=out, in0=in_, scalar1=T["negmean", u][:, j:j + 1], scalar2=rstd,
                                      op0=ALU.add, op1=ALU.mult)

        def transpose_z(u, t0):
            n = UNITS[u]
            if t0 == 0:
                T["planes", u] = work.tile([P, 4, n * P], BF16, tag="planes", bufs=2, name="planes")
            T["z_t", u, t0] = bank("tp")
            for t in range(t0, t0 + 4 // n):
                for j in range(n):
                    c0 = ((t - t0) * n + j) * P
                    nc.tensor.transpose(T["z_t", u, t0][:, c0:c0 + P], T["z", u][:, j, t * P:(t + 1) * P], ident_f[:])

        def gain_bias(u, t0):
            n = UNITS[u]
            for t in range(t0, t0 + 4 // n):
                c0 = (t - t0) * n * P
                nc.scalar.activation(out=T["planes", u][:, t, :], in_=T["z_t", u, t0][:, c0:c0 + n * P],
                                     func=ACT.Identity, bias=gb[:, 4 + t:5 + t], scale=gb[:, t:t + 1])

        def regroup_h2(u):
            T["h_grp", u] = work.tile([P, UNITS[u] * P, 4], BF16, align_bytes=64, tag="h_grp", bufs=2, name="h_grp")
            regroup(T["h_grp", u][:], T["planes", u][:])

        def quantise_h2(u):
            n = UNITS[u]
            T["h_codes", u] = work.tile([P, n * P], U32, align_bytes=64, tag="h_codes", bufs=2, name="h_codes")
            T["h_scl", u] = work.tile([P, n * P], U8, align_bytes=64, tag="h_scl", bufs=2, name="h_scl")
            nc.vector.quantize_mx(out=T["h_codes", u][:].bitcast(FP8X4), scales=T["h_scl", u][:],
                                  in_=T["h_grp", u][:].rearrange("p r t -> p (r t)"))

        def product_2(u):
            n = UNITS[u]
            T["mm2", u] = psum.tile([P, n, F], F32, tag="tp", bufs=3, name="mm2")
            for j in range(n):
                cols = slice(j * P, (j + 1) * P)
                nc.tensor.matmul_mx(out=T["mm2", u][:, j, :], lhsT=T["h_codes", u][:, cols].bitcast(FP8X4),
                                    lhsT_scale=T["h_scl", u][:, cols], rhs=w1_codes[:].bitcast(FP8X4),
                                    rhs_scale=w1_scl[:], start=True, stop=True)

        def add_b1(u):
            n = UNITS[u]
            T["pre", u] = work.tile([P, n, F], F32, tag="pre", bufs=2, name="pre")
            nc.vector.tensor_tensor(out=T["pre", u][:], in0=T["mm2", u][:], in1=b1_sb[:, 0:n, :], op=ALU.add)

        def gelu(u):
            n = UNITS[u]
            hid = work.tile([P, n, F], F32, tag="hid", bufs=3)
            nc.scalar.activation(out=hid[:], in_=T["pre", u][:], func=ACT.Gelu)
            nc.sync.dma_start(out=hid_v[:, first[u]:first[u] + n, :], in_=hid[:])

        def each(u, f, *indices):
            if 0 <= u < n_units:
                for i in indices:
                    f(u, i)

        def whole(u, f):
            if 0 <= u < n_units:
                f(u)

        def tiles(u):
            return UNITS[u] if 0 <= u < n_units else 0

        for s in range(-3, n_units + 4):
            if s == -2:
                const_b_out()
            if s == 0:
                const_stage_2()
            whole(s - 1, statistics)
            each(s - 1, normalise, "gpsimd", "scalar")
            for j in range(4):
                if j < tiles(s):
                    residual(s, j)
                    squares(s, j)
                if j < tiles(s + 1) and s >= -1:
                    product_1(s + 1, j)
            each(s - 1, normalise, "vector")
            whole(s - 4, add_b1)
            whole(s, store_x_mid)
            if tiles(s - 1):
                values = range(0, 4, 4 // tiles(s - 1))
                each(s - 1, transpose_z, *values[:3])
                each(s - 1, gain_bias, values[0])
                each(s - 1, transpose_z, *values[3:])
                each(s - 1, gain_bias, *values[1:])
            whole(s - 4, gelu)
            for pair in range(tiles(s + 3) // 2):
                transpose_attn(s + 3, pair)
            whole(s - 3, product_2)
            for pair in range(tiles(s + 3) // 2):
                copy_attn(s + 3, pair)
            whole(s - 2, regroup_h2)
            whole(s + 2, quantise_attn)
            whole(s - 2, quantise_h2)
            whole(s + 2, add_b_out)
